import numpy as np
import ml_dtypes


def mxq(x, axis, fmt="e4m3"):
    dtype, down = {"e4m3": (ml_dtypes.float8_e4m3fn, 7), "e5m2": (ml_dtypes.float8_e5m2, 14)}[fmt]
    v = np.moveaxis(np.asarray(x, np.float32).astype(ml_dtypes.bfloat16).astype(np.float64), axis, -1)
    blocks = v.reshape(v.shape[:-1] + (-1, 32))
    amax = np.abs(blocks).max(-1, keepdims=True)
    byte = np.maximum(np.where(amax > 0, np.frexp(amax)[1] - 1 + 127, 0) - down, 1)
    scale = np.exp2(byte - 127.0)
    codes = (blocks / scale).astype(np.float32).astype(dtype).astype(np.float64)
    return np.moveaxis((codes * scale).reshape(v.shape), -1, axis)


WIDE = False


def mx_kscale(k):
    if not WIDE:
        return np.ones(k)
    levels = np.array([10, -10, 5, -5, 0])
    a = np.random.permutation(np.resize(levels, k // 512 * 4)).reshape(k // 512, 4)
    idx = np.arange(k)
    return np.exp2(a[idx // 512, idx % 128 // 32])


BF16 = ml_dtypes.bfloat16


def bf(x):
    return np.asarray(x, np.float32).astype(BF16)


def f64(x):
    return np.asarray(x).astype(np.float64)


B, P, D, DFF = 8, 64, 512, 1024


def sigmoid(v):
    return 1.0 / (1.0 + np.exp(-v))


def setup_inputs():
    s = mx_kscale(D)
    inp = {
        'Zi': bf(np.random.standard_normal((B, P, D)) * s),
        'Ci': bf(np.random.standard_normal((B, P, DFF))),
        'Mi': bf(np.random.standard_normal((B, P, DFF))),
        'Hi': bf(np.random.standard_normal((B, P, DFF))),
        'Ni': bf(np.random.uniform(0.5, 1.5, (B, P, DFF))),
        'm': bf(np.random.uniform(0.0, 1.0, (B, P, 1))),
    }
    for n in ('WI', 'WF', 'WO', 'WZ'):
        inp[n + '_w'] = bf(np.random.standard_normal((DFF, DFF)) * 0.7 / np.sqrt(DFF))
        inp[n + '_b'] = bf(np.random.standard_normal(DFF) * 0.3)
    for n in ('RI', 'RF', 'RO', 'RZ'):
        inp[n + '_w'] = bf(np.random.standard_normal((D, DFF)) * 0.7 / np.sqrt(D) / s[:, None])
        inp[n + '_b'] = bf(np.random.standard_normal(DFF) * 0.3)
    return inp


def reference(Zi, Ci, Mi, Hi, Ni, m,
              WI_w, WI_b, WF_w, WF_b, WO_w, WO_b, WZ_w, WZ_b,
              RI_w, RI_b, RF_w, RF_b, RO_w, RO_b, RZ_w, RZ_b):
    Zi, Ci, Mi, Hi, Ni, m = f64(Zi), f64(Ci), f64(Mi), f64(Hi), f64(Ni), f64(m)
    Wh = np.concatenate([f64(WI_w), f64(WF_w), f64(WO_w), f64(WZ_w)], axis=1)
    Wz = np.concatenate([f64(RI_w), f64(RF_w), f64(RO_w), f64(RZ_w)], axis=1)
    bias = np.concatenate([f64(WI_b) + f64(RI_b), f64(WF_b) + f64(RF_b), f64(WO_b) + f64(RO_b), f64(WZ_b) + f64(RZ_b)])
    gates = (mxq(Hi, 2, 'e4m3') @ mxq(Wh, 0, 'e4m3')) + (mxq(Zi, 2, 'e4m3') @ mxq(Wz, 0, 'e4m3')) + bias
    I_tilde, F_tilde, O_tilde, Z_tilde = np.split(gates, 4, axis=-1)

    M_t = np.maximum(F_tilde + Mi, I_tilde)
    I_t = np.exp(I_tilde - M_t)
    F_t = np.exp(F_tilde + Mi - M_t)
    O_t = sigmoid(O_tilde)
    N_t = F_t * Ni + I_t
    Z_t = np.tanh(Z_tilde)
    C_t = (Ci * F_t + Z_t * I_t) * m + (1.0 - m) * Ci
    H_t = O_t * (C_t / N_t) * m + (1.0 - m) * Hi
    return (C_t, M_t, H_t, N_t)

@@ -1,0 +1,369 @@
+from contextlib import ExitStack
+
+from concourse import mybir
+from concourse.masks import make_identity
+
+F32 = mybir.dt.float32
+BF16 = mybir.dt.bfloat16
+U32 = mybir.dt.uint32
+U8 = mybir.dt.uint8
+FP8X4 = mybir.dt.float8_e4m3fn_x4
+ALU = mybir.AluOpType
+ACT = mybir.ActivationFunctionType
+
+P = 128
+TOK = 512
+NT = 4
+DFF = 1024
+HALF = 512
+FLOPS = 2 * 512 * 1536 * 4096
+
+G_I, G_F, G_O, G_Z = 0, 1, 2, 3
+PAIRS = ((0, 1), (2, 3))
+
+
+def tile_customlstmcell_kernel(
+    tc,
+    Zi, Ci, Mi, Hi, Ni, m,
+    WI_w, WI_b, WF_w, WF_b, WO_w, WO_b, WZ_w, WZ_b,
+    RI_w, RI_b, RF_w, RF_b, RO_w, RO_b, RZ_w, RZ_b,
+    out_0, out_1, out_2, out_3,
+):
+    nc = tc.nc
+    W_of = {G_I: WI_w, G_F: WF_w, G_O: WO_w, G_Z: WZ_w}
+    R_of = {G_I: RI_w, G_F: RF_w, G_O: RO_w, G_Z: RZ_w}
+    biases = [WI_b, WF_b, WO_b, WZ_b, RI_b, RF_b, RO_b, RZ_b]
+
+    def rows(ap):
+        return ap.rearrange("b p k -> (b p) k")
+
+    def tiled(ap):
+        return rows(ap).rearrange("(i q) k -> q i k", q=P)
+
+    C_out, M_out, H_out, N_out = rows(out_0), rows(out_1), rows(out_2), rows(out_3)
+
+    with ExitStack() as ctx:
+        consts = ctx.enter_context(tc.tile_pool(name="consts", bufs=1))
+        keep = ctx.enter_context(tc.tile_pool(name="keep", bufs=1))
+        codes = ctx.enter_context(tc.tile_pool(name="codes", bufs=1))
+        gtp = ctx.enter_context(tc.tile_pool(name="gtp", bufs=8))
+        rawp = ctx.enter_context(tc.tile_pool(name="rawp", bufs=4))
+        statep = ctx.enter_context(tc.tile_pool(name="statep", bufs=1))
+        grpp = ctx.enter_context(tc.tile_pool(name="grpp", bufs=2))
+        planes = ctx.enter_context(tc.tile_pool(name="planes", bufs=1))
+        tmp = ctx.enter_context(tc.tile_pool(name="tmp", bufs=2))
+        psmx = ctx.enter_context(tc.psum_pool(name="psmx", bufs=4))
+        pstp = ctx.enter_context(tc.psum_pool(name="pstp", bufs=4))
+        ctx.enter_context(tc.manual_schedule())
+
+        hi_sb = keep.tile([P, NT, DFF], BF16, name="hi_sb")
+        xq = keep.tile([P, 3, TOK], U32, name="xq", align_bytes=64)
+        xs = keep.tile([P, 3, TOK], U8, name="xs", align_bytes=64)
+        ident = consts.tile([P, P], F32, name="ident")
+        braw = consts.tile([P, P], BF16, name="braw")
+        bf32 = consts.tile([P, P], F32, name="bf32")
+        cst = consts.tile([P, P], F32, name="cst")
+        bsum = consts.tile([P, 32], F32, name="bsum")
+        boh = consts.tile([P, 8], F32, name="boh")
+        om = consts.tile([P, NT], F32, name="om")
+        mh = consts.tile([P, NT], F32, name="mh")
+        e1p = planes.tile([P, 8, HALF], F32, name="e1p")
+        t2p = planes.tile([P, 8, HALF], F32, name="t2p")
+        npl = planes.tile([P, 8, HALF], F32, name="npl")
+        rsp = planes.tile([P, 8, HALF], F32, name="rsp")
+
+        raw, grouped, wq, ws, acc, gt, tp, state, hm = {}, {}, {}, {}, {}, {}, {}, {}, {}
+
+        def m_col(i):
+            return cst[:, 64 + i : 65 + i]
+
+        def col_range(h):
+            return slice(h * HALF, h * HALF + HALF)
+
+        def tok_range(i):
+            return slice(i * P, i * P + P)
+
+        def load_x():
+            nc.sync.dma_start(out=hi_sb[:], in_=tiled(Hi))
+            raw["zi"] = rawp.tile([P, NT, 512], BF16, tag="raw", name="zi_sb")
+            nc.sync.dma_start(out=raw["zi"][:], in_=tiled(Zi))
+            make_identity(nc, ident[:])
+            nc.vector.memset(braw[:], 0.0)
+            for v, b in enumerate(biases):
+                nc.scalar.dma_start(out=braw[8 * v : 8 * v + 8, :], in_=b.rearrange("(r c) -> r c", c=P))
+            nc.scalar.dma_start(out=braw[64:68, :], in_=m.rearrange("(r x) p o -> r (x p o)", x=2))
+
+        def prepare_x():
+            hi_w = hi_sb[:].rearrange("q i k -> q (i k)").bitcast(F32).rearrange("q (n w u) -> q n w u", w=P, u=2)
+            zi_w = raw["zi"][:].rearrange("q i k -> q (i k)").bitcast(F32).rearrange("q (n w u) -> q n w u", w=P, u=2)
+            xg = {}
+            for c in range(3):
+                xg[c] = grpp.tile([P, 2, 1024], BF16, tag="grouped", name="xg", align_bytes=64)
+                for hh in range(2):
+                    xt = pstp.tile([P, 512], F32, tag="tp", name="xt")
+                    for u in range(2):
+                        for il in range(2):
+                            i = 2 * hh + il
+                            src = hi_w[:, 2 * i + c, :, u] if c < 2 else zi_w[:, i, :, u]
+                            nc.tensor.transpose(xt[:, u * 256 + il * P : u * 256 + il * P + P], src, ident[:])
+                    dst = xg[c][:, hh, :].bitcast(F32).rearrange("p (r u) -> p r u", u=2)
+                    view = xt[:].rearrange("p (u r) -> p r u", u=2)
+                    if hh == 0:
+                        nc.vector.tensor_copy(out=dst, in_=view)
+                    else:
+                        nc.scalar.copy(out=dst, in_=view)
+                if c > 0:
+                    quantise_x(xg, c - 1)
+            quantise_x(xg, 2)
+
+        def quantise_x(xg, c):
+            nc.vector.quantize_mx(out=xq[:, c, :].bitcast(FP8X4), scales=xs[:, c, :], in_=xg[c][:].rearrange("p a b -> p (a b)"))
+
+        def prepare_consts():
+            nc.vector.tensor_copy(out=bf32[:], in_=braw[:])
+            bt = pstp.tile([P, 512], F32, tag="tp", name="bt")
+            nc.tensor.transpose(bt[:, 0:P], bf32[:], ident[:])
+            nc.vector.tensor_copy(out=cst[:], in_=bt[:, 0:P])
+            nc.vector.tensor_tensor(out=bsum[:], in0=cst[:, 0:32], in1=cst[:, 32:64], op=ALU.add)
+            nc.vector.tensor_scalar(out=om[:], in0=cst[:, 64:68], scalar1=-1.0, scalar2=1.0, op0=ALU.mult, op1=ALU.add)
+            nc.vector.tensor_scalar(out=mh[:], in0=cst[:, 64:68], scalar1=0.5, scalar2=None, op0=ALU.mult)
+            nc.vector.tensor_scalar(out=boh[:], in0=bsum[:, 8 * G_O : 8 * G_O + 8], scalar1=0.5, scalar2=None, op0=ALU.mult)
+
+        def load_slab(g, c):
+            src = W_of[g][512 * c : 512 * c + 512, :] if c < 2 else R_of[g]
+            raw[(g, c)] = rawp.tile([P, 4, DFF], BF16, tag="raw", name="raw")
+            nc.sync.dma_start(out=raw[(g, c)][:], in_=src.rearrange("(p j) w -> p j w", j=4))
+
+        def regroup(g, c, second):
+            grouped[(g, c)] = grpp.tile([P, DFF, 4], BF16, tag="grouped", name="grouped", align_bytes=64)
+            for hh in range(2):
+                dst = grouped[(g, c)][:, hh * HALF : hh * HALF + HALF, :].rearrange("p (c i) t -> p c t i", i=4)
+                view = raw[(g, c)][:, :, hh * HALF : hh * HALF + HALF].rearrange("p t (c i) -> p c t i", i=4)
+                if hh == 1 and second == "S":
+                    nc.scalar.copy(out=dst, in_=view)
+                else:
+                    nc.vector.tensor_copy(out=dst, in_=view)
+
+        def quantise(g, c):
+            wq[(g, c)] = codes.tile([P, DFF], U32, name="wq%d_%d" % (g, c), align_bytes=64)
+            ws[(g, c)] = codes.tile([P, DFF], U8, name="ws%d_%d" % (g, c), align_bytes=64)
+            nc.vector.quantize_mx(
+                out=wq[(g, c)][:].bitcast(FP8X4), scales=ws[(g, c)][:], in_=grouped[(g, c)][:].rearrange("p w j -> p (w j)"))
+
+        def load_state(ap, h, name):
+            state[(name, h)] = statep.tile([P, NT, HALF], BF16, tag=name, name=name)
+            nc.sync.dma_start(out=state[(name, h)][:], in_=tiled(ap)[:, :, col_range(h)])
+
+        def products(g, h):
+            acc[(g, h)] = []
+            for cbl in range(4):
+                cols = slice((4 * h + cbl) * P, (4 * h + cbl) * P + P)
+                a = psmx.tile([P, TOK], F32, tag="mx", name="a")
+                for c in range(3):
+                    nc.tensor.matmul_mx(
+                        out=a[:],
+                        lhsT=wq[(g, c)][:, cols].bitcast(FP8X4),
+                        lhsT_scale=ws[(g, c)][:, cols],
+                        rhs=xq[:, c, :].bitcast(FP8X4),
+                        rhs_scale=xs[:, c, :],
+                        start=(c == 0),
+                        stop=(c == 2),
+                    )
+                acc[(g, h)].append(a)
+
+        def leave(g, h):
+            gt[(g, h)] = []
+            for cbl in range(4):
+                cb = 4 * h + cbl
+                t = gtp.tile([P, TOK], F32, tag="gt", name="t")
+                if g == G_O:
+                    nc.scalar.activation(out=t[:], in_=acc[(g, h)][cbl][:], func=ACT.Tanh, bias=boh[:, cb : cb + 1], scale=0.5)
+                else:
+                    func = ACT.Tanh if g == G_Z else ACT.Identity
+                    nc.scalar.activation(out=t[:], in_=acc[(g, h)][cbl][:], func=func, bias=bsum[:, 8 * g + cb : 8 * g + cb + 1], scale=1.0)
+                gt[(g, h)].append(t)
+
+        def back(g, h):
+            tp[(g, h)] = []
+            for i in range(NT):
+                t = pstp.tile([P, HALF], F32, tag="tp", name="t")
+                for cbl in range(4):
+                    nc.tensor.transpose(t[:, cbl * P : cbl * P + P], gt[(g, h)][cbl][:, tok_range(i)], ident[:])
+                tp[(g, h)].append(t)
+
+        def cell_b(h):
+            for i in range(NT):
+                nc.vector.tensor_tensor(out=e1p[:, 4 * h + i, :], in0=tp[(G_F, h)][i][:], in1=state[("mi", h)][:, i, :], op=ALU.add)
+
+        def cell_md(h):
+            for i in range(NT):
+                x = 4 * h + i
+                nc.vector.tensor_tensor(out=rsp[:, x, :], in0=tp[(G_I, h)][i][:], in1=e1p[:, x, :], op=ALU.max)
+                nc.sync.dma_start(out=M_out[tok_range(i), col_range(h)], in_=rsp[:, x, :])
+                nc.vector.tensor_tensor(out=t2p[:, x, :], in0=tp[(G_I, h)][i][:], in1=e1p[:, x, :], op=ALU.subtract)
+
+        def cell_exp(h, tiles):
+            for i in tiles:
+                x = 4 * h + i
+                nc.scalar.activation(out=e1p[:, x, :], in_=t2p[:, x, :], func=ACT.Exp)
+                nc.scalar.activation(out=npl[:, x, :], in_=t2p[:, x, :], func=ACT.Exp, scale=-1.0)
+
+        def cell_n(h, pair):
+            t1, gm = {}, {}
+            for i in pair:
+                t1[i] = tmp.tile([P, HALF], F32, tag="ta", name="t1")
+                nc.vector.scalar_tensor_tensor(out=t1[i][:], in0=npl[:, 4 * h + i, :], scalar=1.0, in1=state[("ni", h)][:, i, :], op0=ALU.min, op1=ALU.mult)
+            for i in pair:
+                gm[i] = tmp.tile([P, HALF], F32, tag="tb", name="gm")
+                nc.vector.tensor_scalar(out=gm[i][:], in0=npl[:, 4 * h + i, :], scalar1=1.0, scalar2=m_col(i), op0=ALU.min, op1=ALU.mult)
+            for i in pair:
+                x = 4 * h + i
+                nc.vector.scalar_tensor_tensor(out=npl[:, x, :], in0=e1p[:, x, :], scalar=1.0, in1=t1[i][:], op0=ALU.min, op1=ALU.add)
+                nc.sync.dma_start(out=N_out[tok_range(i), col_range(h)], in_=npl[:, x, :])
+            for i in pair:
+                nc.vector.scalar_tensor_tensor(out=t2p[:, 4 * h + i, :], in0=gm[i][:], scalar=om[:, i : i + 1], in1=state[("ci", h)][:, i, :], op0=ALU.add, op1=ALU.mult)
+
+        def cell_abs(h, tiles):
+            for i in tiles:
+                nc.scalar.activation(out=rsp[:, 4 * h + i, :], in_=npl[:, 4 * h + i, :], func=ACT.Abs)
+
+        def half_plane(t, h):
+            return t[:, 4 * h : 4 * h + 4, :].rearrange("p a b -> p (a b)")
+
+        def recip_ln(h):
+            nc.scalar.activation(out=half_plane(rsp, h), in_=half_plane(rsp, h), func=ACT.Ln)
+
+        def recip_exp(h):
+            nc.scalar.activation(out=half_plane(rsp, h), in_=half_plane(rsp, h), func=ACT.Exp, scale=-2.0)
+
+        def recip_sign(h):
+            nc.vector.tensor_tensor(out=half_plane(rsp, h), in0=half_plane(rsp, h), in1=half_plane(npl, h), op=ALU.mult)
+
+        def cell_c(h, pair):
+            t3 = {}
+            for i in pair:
+                t3[i] = tmp.tile([P, HALF], F32, tag="ta", name="t3")
+                nc.vector.scalar_tensor_tensor(out=t3[i][:], in0=e1p[:, 4 * h + i, :], scalar=1.0, in1=tp[(G_Z, h)][i][:], op0=ALU.min, op1=ALU.mult)
+            for i in pair:
+                x = 4 * h + i
+                nc.vector.scalar_tensor_tensor(out=npl[:, x, :], in0=t3[i][:], scalar=m_col(i), in1=t2p[:, x, :], op0=ALU.mult, op1=ALU.add)
+                nc.sync.dma_start(out=C_out[tok_range(i), col_range(h)], in_=npl[:, x, :])
+            for i in pair:
+                x = 4 * h + i
+                nc.vector.tensor_tensor(out=t2p[:, x, :], in0=npl[:, x, :], in1=rsp[:, x, :], op=ALU.mult)
+
+        def cell_hm(h, tiles):
+            for i in tiles:
+                hm[(h, i)] = tmp.tile([P, HALF], F32, tag="tc", name="hm", bufs=4)
+                nc.scalar.activation(out=hm[(h, i)][:], in_=hi_sb[:, i, col_range(h)], func=ACT.Copy, scale=om[:, i : i + 1])
+
+        def cell_h(h, pair):
+            y2 = {}
+            for i in pair:
+                y2[i] = tmp.tile([P, HALF], F32, tag="tb", name="y2")
+                nc.vector.scalar_tensor_tensor(out=y2[i][:], in0=tp[(G_O, h)][i][:], scalar=1.0, in1=t2p[:, 4 * h + i, :], op0=ALU.add, op1=ALU.mult)
+            for i in pair:
+                x = 4 * h + i
+                nc.vector.scalar_tensor_tensor(out=e1p[:, x, :], in0=y2[i][:], scalar=mh[:, i : i + 1], in1=hm[(h, i)][:], op0=ALU.mult, op1=ALU.add)
+                nc.sync.dma_start(out=H_out[tok_range(i), col_range(h)], in_=e1p[:, x, :])
+
+        F, I, Z, O = G_F, G_I, G_Z, G_O
+        load_x()
+        for c in range(3):
+            load_slab(F, c)
+        prepare_x()
+        load_slab(I, 0)
+
+        regroup(F, 0, "S")
+        load_slab(I, 1)
+        regroup(F, 1, "S")
+        load_slab(I, 2)
+        quantise(F, 0)
+        prepare_consts()
+        regroup(F, 2, "S")
+        load_slab(Z, 0)
+        quantise(F, 1)
+        regroup(I, 0, "S")
+        load_state(Mi, 0, "mi")
+        load_slab(Z, 1)
+        quantise(F, 2)
+        products(F, 0)
+        regroup(I, 1, "S")
+        load_state(Ni, 0, "ni")
+        load_state(Ci, 0, "ci")
+        load_slab(Z, 2)
+        quantise(I, 0)
+        leave(F, 0)
+        regroup(I, 2, "S")
+        load_slab(O, 0)
+        quantise(I, 1)
+        back(F, 0)
+        regroup(Z, 0, "S")
+        load_slab(O, 1)
+        quantise(I, 2)
+        products(I, 0)
+        leave(I, 0)
+        cell_b(0)
+        back(I, 0)
+        regroup(Z, 1, "S")
+        load_slab(O, 2)
+        quantise(Z, 0)
+        products(F, 1)
+        leave(F, 1)
+        cell_md(0)
+        load_state(Mi, 1, "mi")
+        cell_exp(0, (0, 1, 2, 3))
+        regroup(Z, 2, "V")
+        quantise(Z, 1)
+        back(F, 1)
+        products(I, 1)
+        leave(I, 1)
+        cell_n(0, (0, 1))
+        cell_abs(0, (0, 1))
+        cell_n(0, (2, 3))
+        cell_abs(0, (2, 3))
+        load_state(Ni, 1, "ni")
+        load_state(Ci, 1, "ci")
+        quantise(Z, 2)
+        cell_b(1)
+        back(I, 1)
+        recip_ln(0)
+        regroup(O, 0, "S")
+        cell_md(1)
+        recip_exp(0)
+        cell_exp(1, (0, 1, 2, 3))
+        regroup(O, 1, "S")
+        quantise(O, 0)
+        products(Z, 0)
+        leave(Z, 0)
+        recip_sign(0)
+        cell_n(1, (0, 1))
+        cell_abs(1, (0, 1))
+        regroup(O, 2, "V")
+        quantise(O, 1)
+        cell_n(1, (2, 3))
+        cell_abs(1, (2, 3))
+        back(Z, 0)
+        quantise(O, 2)
+        products(O, 0)
+        recip_ln(1)
+        cell_c(0, (0, 1))
+        cell_c(0, (2, 3))
+        leave(O, 0)
+        cell_hm(0, (0, 1, 2, 3))
+        recip_exp(1)
+        back(O, 0)
+        products(Z, 1)
+        leave(Z, 1)
+        cell_h(0, (0, 1))
+        cell_h(0, (2, 3))
+        recip_sign(1)
+        back(Z, 1)
+        products(O, 1)
+        leave(O, 1)
+        cell_hm(1, (0, 1, 2, 3))
+        cell_c(1, (0, 1))
+        cell_c(1, (2, 3))
+        back(O, 1)
+        cell_h(1, (0, 1))
+        cell_h(1, (2, 3))

@@ -87,6 +87,8 @@ def tile_customlstmcell_kernel(
             nc.sync.dma_start(out=hi_sb[:], in_=tiled(Hi))
             raw["zi"] = rawp.tile([P, NT, 512], BF16, tag="raw", name="zi_sb")
             nc.sync.dma_start(out=raw["zi"][:], in_=tiled(Zi))
+
+        def load_consts():
             make_identity(nc, ident[:])
             nc.vector.memset(braw[:], 0.0)
             for v, b in enumerate(biases):
@@ -129,10 +131,13 @@ def tile_customlstmcell_kernel(
             nc.vector.tensor_scalar(out=mh[:], in0=cst[:, 64:68], scalar1=0.5, scalar2=None, op0=ALU.mult)
             nc.vector.tensor_scalar(out=boh[:], in0=bsum[:, 8 * G_O : 8 * G_O + 8], scalar1=0.5, scalar2=None, op0=ALU.mult)
 
-        def load_slab(g, c):
+        def load_slab(g, c, pieces=1):
             src = W_of[g][512 * c : 512 * c + 512, :] if c < 2 else R_of[g]
             raw[(g, c)] = rawp.tile([P, 4, DFF], BF16, tag="raw", name="raw")
-            nc.sync.dma_start(out=raw[(g, c)][:], in_=src.rearrange("(p j) w -> p j w", j=4))
+            width = DFF // pieces
+            for k in range(pieces):
+                cols = slice(k * width, k * width + width)
+                nc.sync.dma_start(out=raw[(g, c)][:, :, cols], in_=src.rearrange("(p j) w -> p j w", j=4)[:, :, cols])
 
         def regroup(g, c, second):
             grouped[(g, c)] = grpp.tile([P, DFF, 4], BF16, tag="grouped", name="grouped", align_bytes=64)
@@ -236,9 +241,6 @@ def tile_customlstmcell_kernel(
         def recip_exp(h):
             nc.scalar.activation(out=half_plane(rsp, h), in_=half_plane(rsp, h), func=ACT.Exp, scale=-2.0)
 
-        def recip_sign(h):
-            nc.vector.tensor_tensor(out=half_plane(rsp, h), in0=half_plane(rsp, h), in1=half_plane(npl, h), op=ALU.mult)
-
         def cell_c(h, pair):
             t3 = {}
             for i in pair:
@@ -246,11 +248,16 @@ def tile_customlstmcell_kernel(
                 nc.vector.scalar_tensor_tensor(out=t3[i][:], in0=e1p[:, 4 * h + i, :], scalar=1.0, in1=tp[(G_Z, h)][i][:], op0=ALU.min, op1=ALU.mult)
             for i in pair:
                 x = 4 * h + i
-                nc.vector.scalar_tensor_tensor(out=npl[:, x, :], in0=t3[i][:], scalar=m_col(i), in1=t2p[:, x, :], op0=ALU.mult, op1=ALU.add)
-                nc.sync.dma_start(out=C_out[tok_range(i), col_range(h)], in_=npl[:, x, :])
+                nc.vector.scalar_tensor_tensor(out=e1p[:, x, :], in0=t3[i][:], scalar=m_col(i), in1=t2p[:, x, :], op0=ALU.mult, op1=ALU.add)
+                nc.sync.dma_start(out=C_out[tok_range(i), col_range(h)], in_=e1p[:, x, :])
             for i in pair:
                 x = 4 * h + i
-                nc.vector.tensor_tensor(out=t2p[:, x, :], in0=npl[:, x, :], in1=rsp[:, x, :], op=ALU.mult)
+                nc.vector.tensor_tensor(out=t2p[:, x, :], in0=e1p[:, x, :], in1=npl[:, x, :], op=ALU.mult)
+
+        def cell_o(h):
+            for i in range(NT):
+                x = 4 * h + i
+                nc.vector.scalar_tensor_tensor(out=t2p[:, x, :], in0=tp[(G_O, h)][i][:], scalar=1.0, in1=t2p[:, x, :], op0=ALU.add, op1=ALU.mult)
 
         def cell_hm(h, tiles):
             for i in tiles:
@@ -258,112 +265,104 @@ def tile_customlstmcell_kernel(
                 nc.scalar.activation(out=hm[(h, i)][:], in_=hi_sb[:, i, col_range(h)], func=ACT.Copy, scale=om[:, i : i + 1])
 
         def cell_h(h, pair):
-            y2 = {}
+            y = {}
             for i in pair:
-                y2[i] = tmp.tile([P, HALF], F32, tag="tb", name="y2")
-                nc.vector.scalar_tensor_tensor(out=y2[i][:], in0=tp[(G_O, h)][i][:], scalar=1.0, in1=t2p[:, 4 * h + i, :], op0=ALU.add, op1=ALU.mult)
+                y[i] = tmp.tile([P, HALF], F32, tag="tb", name="y")
+                nc.vector.tensor_tensor(out=y[i][:], in0=t2p[:, 4 * h + i, :], in1=rsp[:, 4 * h + i, :], op=ALU.mult)
             for i in pair:
                 x = 4 * h + i
-                nc.vector.scalar_tensor_tensor(out=e1p[:, x, :], in0=y2[i][:], scalar=mh[:, i : i + 1], in1=hm[(h, i)][:], op0=ALU.mult, op1=ALU.add)
-                nc.sync.dma_start(out=H_out[tok_range(i), col_range(h)], in_=e1p[:, x, :])
+                nc.vector.scalar_tensor_tensor(out=npl[:, x, :], in0=y[i][:], scalar=mh[:, i : i + 1], in1=hm[(h, i)][:], op0=ALU.mult, op1=ALU.add)
+                nc.sync.dma_start(out=H_out[tok_range(i), col_range(h)], in_=npl[:, x, :])
 
         F, I, Z, O = G_F, G_I, G_Z, G_O
-        load_x()
-        for c in range(3):
-            load_slab(F, c)
-        prepare_x()
-        load_slab(I, 0)
+        state_of = {"mi": Mi, "ni": Ni, "ci": Ci}
+        loads = [(F, 0), (F, 1), (F, 2), (I, 0), (I, 1), (I, 2), (Z, 0), ("mi", 0), (Z, 1), ("ni", 0), ("ci", 0), (Z, 2), (O, 0), (O, 1), (O, 2)]
+        slabs = [(g, c) for g in (F, I, Z, O) for c in range(3)]
+        waiting = []
 
-        regroup(F, 0, "S")
-        load_slab(I, 1)
-        regroup(F, 1, "S")
-        load_slab(I, 2)
-        quantise(F, 0)
+        def next_load():
+            while loads:
+                what, k = loads.pop(0)
+                if what in state_of:
+                    load_state(state_of[what], k, what)
+                else:
+                    load_slab(what, k)
+                    break
+
+        def next_slab():
+            if slabs:
+                g, c = slabs.pop(0)
+                regroup(g, c, "S")
+                next_load()
+                waiting.append((g, c))
+            if len(waiting) > 1 or not slabs:
+                g, c = waiting.pop(0)
+                quantise(g, c)
+
+        load_consts()
+        load_x()
+        for k in range(3):
+            next_load()
+        prepare_x()
+        next_load()
+        next_slab()
+        next_slab()
         prepare_consts()
-        regroup(F, 2, "S")
-        load_slab(Z, 0)
-        quantise(F, 1)
-        regroup(I, 0, "S")
-        load_state(Mi, 0, "mi")
-        load_slab(Z, 1)
-        quantise(F, 2)
+        next_slab()
+        next_slab()
         products(F, 0)
-        regroup(I, 1, "S")
-        load_state(Ni, 0, "ni")
-        load_state(Ci, 0, "ci")
-        load_slab(Z, 2)
-        quantise(I, 0)
+        next_slab()
         leave(F, 0)
-        regroup(I, 2, "S")
-        load_slab(O, 0)
-        quantise(I, 1)
+        next_slab()
         back(F, 0)
-        regroup(Z, 0, "S")
-        load_slab(O, 1)
-        quantise(I, 2)
+        next_slab()
         products(I, 0)
         leave(I, 0)
-        cell_b(0)
-        back(I, 0)
-        regroup(Z, 1, "S")
-        load_slab(O, 2)
-        quantise(Z, 0)
-        products(F, 1)
-        leave(F, 1)
-        cell_md(0)
-        load_state(Mi, 1, "mi")
-        cell_exp(0, (0, 1, 2, 3))
-        regroup(Z, 2, "V")
-        quantise(Z, 1)
-        back(F, 1)
-        products(I, 1)
-        leave(I, 1)
-        cell_n(0, (0, 1))
-        cell_abs(0, (0, 1))
-        cell_n(0, (2, 3))
-        cell_abs(0, (2, 3))
-        load_state(Ni, 1, "ni")
-        load_state(Ci, 1, "ci")
-        quantise(Z, 2)
-        cell_b(1)
-        back(I, 1)
-        recip_ln(0)
-        regroup(O, 0, "S")
-        cell_md(1)
-        recip_exp(0)
-        cell_exp(1, (0, 1, 2, 3))
-        regroup(O, 1, "S")
-        quantise(O, 0)
-        products(Z, 0)
-        leave(Z, 0)
-        recip_sign(0)
-        cell_n(1, (0, 1))
-        cell_abs(1, (0, 1))
-        regroup(O, 2, "V")
-        quantise(O, 1)
-        cell_n(1, (2, 3))
-        cell_abs(1, (2, 3))
-        back(Z, 0)
-        quantise(O, 2)
+
+        for h in range(2):
+            first, second = ((F, 1), (I, 1)) if h == 0 else ((Z, 0), (Z, 1))
+            cell_b(h)
+            if h == 0:
+                load_state(Mi, 1, "mi")
+            back(I, h)
+            next_slab()
+            products(first[0], first[1])
+            leave(first[0], first[1])
+            cell_md(h)
+            cell_exp(h, (0, 1, 2, 3))
+            next_slab()
+            back(first[0], first[1])
+            products(second[0], second[1])
+            leave(second[0], second[1])
+            cell_n(h, (0, 1))
+            cell_abs(h, (0, 1))
+            next_slab()
+            cell_n(h, (2, 3))
+            cell_abs(h, (2, 3))
+            if h == 0:
+                load_state(Ni, 1, "ni")
+                load_state(Ci, 1, "ci")
+
         products(O, 0)
-        recip_ln(1)
         cell_c(0, (0, 1))
-        cell_c(0, (2, 3))
         leave(O, 0)
-        cell_hm(0, (0, 1, 2, 3))
-        recip_exp(1)
-        back(O, 0)
-        products(Z, 1)
-        leave(Z, 1)
-        cell_h(0, (0, 1))
-        cell_h(0, (2, 3))
-        recip_sign(1)
+        cell_c(0, (2, 3))
         back(Z, 1)
         products(O, 1)
-        leave(O, 1)
-        cell_hm(1, (0, 1, 2, 3))
+        recip_ln(0)
+        recip_ln(1)
         cell_c(1, (0, 1))
         cell_c(1, (2, 3))
+        back(O, 0)
+        cell_hm(0, (0, 1, 2, 3))
+        recip_exp(0)
+        leave(O, 1)
+        recip_exp(1)
+        cell_o(0)
         back(O, 1)
+        cell_h(0, (0, 1))
+        cell_h(0, (2, 3))
+        cell_hm(1, (0, 1, 2, 3))
+        cell_o(1)
         cell_h(1, (0, 1))
         cell_h(1, (2, 3))

@@ -67,12 +67,14 @@ def tile_customlstmcell_kernel(
         boh = consts.tile([P, 8], F32, name="boh")
         om = consts.tile([P, NT], F32, name="om")
         mh = consts.tile([P, NT], F32, name="mh")
+        nbf = consts.tile([P, 8], F32, name="nbf")
+        neg_bf = consts.tile([P, P], BF16, name="neg_bf")
         e1p = planes.tile([P, 8, HALF], F32, name="e1p")
         t2p = planes.tile([P, 8, HALF], F32, name="t2p")
         npl = planes.tile([P, 8, HALF], F32, name="npl")
         rsp = planes.tile([P, 8, HALF], F32, name="rsp")
 
-        raw, grouped, wq, ws, acc, gt, tp, state, hm = {}, {}, {}, {}, {}, {}, {}, {}, {}
+        raw, grouped, wq, ws, acc, gt, tp, state, hm, dif, tpi = {}, {}, {}, {}, {}, {}, {}, {}, {}, {}, {}
 
         def m_col(i):
             return cst[:, 64 + i : 65 + i]
@@ -130,6 +132,8 @@ def tile_customlstmcell_kernel(
             nc.vector.tensor_scalar(out=om[:], in0=cst[:, 64:68], scalar1=-1.0, scalar2=1.0, op0=ALU.mult, op1=ALU.add)
             nc.vector.tensor_scalar(out=mh[:], in0=cst[:, 64:68], scalar1=0.5, scalar2=None, op0=ALU.mult)
             nc.vector.tensor_scalar(out=boh[:], in0=bsum[:, 8 * G_O : 8 * G_O + 8], scalar1=0.5, scalar2=None, op0=ALU.mult)
+            nc.vector.tensor_scalar(out=nbf[:], in0=bsum[:, 8 * G_F : 8 * G_F + 8], scalar1=-1.0, scalar2=None, op0=ALU.mult)
+            nc.vector.tensor_scalar(out=neg_bf[:], in0=ident[:], scalar1=-1.0, scalar2=None, op0=ALU.mult)
 
         def load_slab(g, c, pieces=1):
             src = W_of[g][512 * c : 512 * c + 512, :] if c < 2 else R_of[g]
@@ -183,6 +187,8 @@ def tile_customlstmcell_kernel(
                 t = gtp.tile([P, TOK], F32, tag="gt", name="t")
                 if g == G_O:
                     nc.scalar.activation(out=t[:], in_=acc[(g, h)][cbl][:], func=ACT.Tanh, bias=boh[:, cb : cb + 1], scale=0.5)
+                elif g == G_F:
+                    nc.scalar.activation(out=t[:], in_=acc[(g, h)][cbl][:], func=ACT.Identity, bias=nbf[:, cb : cb + 1], scale=-1.0)
                 else:
                     func = ACT.Tanh if g == G_Z else ACT.Identity
                     nc.scalar.activation(out=t[:], in_=acc[(g, h)][cbl][:], func=func, bias=bsum[:, 8 * g + cb : 8 * g + cb + 1], scale=1.0)
@@ -196,22 +202,37 @@ def tile_customlstmcell_kernel(
                     nc.tensor.transpose(t[:, cbl * P : cbl * P + P], gt[(g, h)][cbl][:, tok_range(i)], ident[:])
                 tp[(g, h)].append(t)
 
-        def cell_b(h):
-            for i in range(NT):
-                nc.vector.tensor_tensor(out=e1p[:, 4 * h + i, :], in0=tp[(G_F, h)][i][:], in1=state[("mi", h)][:, i, :], op=ALU.add)
+        def difference(h, tiles):
+            for i in tiles:
+                t = pstp.tile([P, HALF], F32, tag="tp", name="t")
+                for cbl in range(4):
+                    cols = slice(cbl * P, cbl * P + P)
+                    nc.tensor.matmul(out=t[:, cols], lhsT=gt[(G_I, h)][cbl][:, tok_range(i)], rhs=ident[:], is_transpose=True, start=True, stop=False)
+                    nc.tensor.matmul(out=t[:, cols], lhsT=gt[(G_F, h)][cbl][:, tok_range(i)], rhs=ident[:], is_transpose=True, start=False, stop=False)
+                    nc.tensor.matmul(out=t[:, cols], lhsT=neg_bf[:], rhs=state[("mi", h)][:, i, cols], start=False, stop=True)
+                dif[(h, i)] = t
 
-        def cell_md(h):
-            for i in range(NT):
-                x = 4 * h + i
-                nc.vector.tensor_tensor(out=rsp[:, x, :], in0=tp[(G_I, h)][i][:], in1=e1p[:, x, :], op=ALU.max)
-                nc.sync.dma_start(out=M_out[tok_range(i), col_range(h)], in_=rsp[:, x, :])
-                nc.vector.tensor_tensor(out=t2p[:, x, :], in0=tp[(G_I, h)][i][:], in1=e1p[:, x, :], op=ALU.subtract)
+        def back_tiles(g, h, tiles):
+            for i in tiles:
+                t = pstp.tile([P, HALF], F32, tag="tp", name="t")
+                for cbl in range(4):
+                    nc.tensor.transpose(t[:, cbl * P : cbl * P + P], gt[(g, h)][cbl][:, tok_range(i)], ident[:])
+                tpi[(g, h, i)] = t
 
         def cell_exp(h, tiles):
             for i in tiles:
                 x = 4 * h + i
-                nc.scalar.activation(out=e1p[:, x, :], in_=t2p[:, x, :], func=ACT.Exp)
-                nc.scalar.activation(out=npl[:, x, :], in_=t2p[:, x, :], func=ACT.Exp, scale=-1.0)
+                nc.scalar.activation(out=t2p[:, x, :], in_=dif[(h, i)][:], func=ACT.Relu, scale=-1.0)
+                nc.scalar.activation(out=npl[:, x, :], in_=dif[(h, i)][:], func=ACT.Exp, scale=-1.0)
+            for i in tiles:
+                x = 4 * h + i
+                nc.scalar.activation(out=e1p[:, x, :], in_=t2p[:, x, :], func=ACT.Exp, scale=-1.0)
+
+        def cell_m(h, tiles):
+            for i in tiles:
+                x = 4 * h + i
+                nc.vector.tensor_tensor(out=rsp[:, x, :], in0=tpi[(G_I, h, i)][:], in1=t2p[:, x, :], op=ALU.add)
+                nc.sync.dma_start(out=M_out[tok_range(i), col_range(h)], in_=rsp[:, x, :])
 
         def cell_n(h, pair):
             t1, gm = {}, {}
@@ -279,6 +300,7 @@ def tile_customlstmcell_kernel(
         loads = [(F, 0), (F, 1), (F, 2), (I, 0), (I, 1), (I, 2), (Z, 0), ("mi", 0), (Z, 1), ("ni", 0), ("ci", 0), (Z, 2), (O, 0), (O, 1), (O, 2)]
         slabs = [(g, c) for g in (F, I, Z, O) for c in range(3)]
         waiting = []
+        by_vector = ((Z, 1), (O, 1))
 
         def next_load():
             while loads:
@@ -292,7 +314,7 @@ def tile_customlstmcell_kernel(
         def next_slab():
             if slabs:
                 g, c = slabs.pop(0)
-                regroup(g, c, "S")
+                regroup(g, c, "V" if (g, c) in by_vector else "S")
                 next_load()
                 waiting.append((g, c))
             if len(waiting) > 1 or not slabs:
@@ -314,35 +336,37 @@ def tile_customlstmcell_kernel(
         next_slab()
         leave(F, 0)
         next_slab()
-        back(F, 0)
         next_slab()
         products(I, 0)
         leave(I, 0)
 
         for h in range(2):
             first, second = ((F, 1), (I, 1)) if h == 0 else ((Z, 0), (Z, 1))
-            cell_b(h)
+            difference(h, (0, 1))
+            back_tiles(I, h, (0, 1))
+            cell_exp(h, (0, 1))
+            next_slab()
+            cell_m(h, (0, 1))
+            difference(h, (2, 3))
+            back_tiles(I, h, (2, 3))
+            cell_exp(h, (2, 3))
             if h == 0:
                 load_state(Mi, 1, "mi")
-            back(I, h)
             next_slab()
             products(first[0], first[1])
             leave(first[0], first[1])
-            cell_md(h)
-            cell_exp(h, (0, 1, 2, 3))
-            next_slab()
-            back(first[0], first[1])
-            products(second[0], second[1])
-            leave(second[0], second[1])
             cell_n(h, (0, 1))
             cell_abs(h, (0, 1))
             next_slab()
+            cell_m(h, (2, 3))
+            products(second[0], second[1])
+            leave(second[0], second[1])
             cell_n(h, (2, 3))
             cell_abs(h, (2, 3))
             if h == 0:
                 load_state(Ni, 1, "ni")
                 load_state(Ci, 1, "ci")
-
+        back(Z, 0)
         products(O, 0)
         cell_c(0, (0, 1))
         leave(O, 0)

@@ -49,7 +49,7 @@ def tile_customlstmcell_kernel(
         gtp = ctx.enter_context(tc.tile_pool(name="gtp", bufs=8))
         rawp = ctx.enter_context(tc.tile_pool(name="rawp", bufs=4))
         statep = ctx.enter_context(tc.tile_pool(name="statep", bufs=1))
-        grpp = ctx.enter_context(tc.tile_pool(name="grpp", bufs=2))
+        grpp = ctx.enter_context(tc.tile_pool(name="grpp", bufs=3))
         planes = ctx.enter_context(tc.tile_pool(name="planes", bufs=1))
         tmp = ctx.enter_context(tc.tile_pool(name="tmp", bufs=2))
         psmx = ctx.enter_context(tc.psum_pool(name="psmx", bufs=4))
@@ -69,6 +69,8 @@ def tile_customlstmcell_kernel(
         mh = consts.tile([P, NT], F32, name="mh")
         nbf = consts.tile([P, 8], F32, name="nbf")
         neg_bf = consts.tile([P, P], BF16, name="neg_bf")
+        one_bf = consts.tile([P, P], BF16, name="one_bf")
+        neg_m = consts.tile([P, NT, P], BF16, name="neg_m")
         e1p = planes.tile([P, 8, HALF], F32, name="e1p")
         t2p = planes.tile([P, 8, HALF], F32, name="t2p")
         npl = planes.tile([P, 8, HALF], F32, name="npl")
@@ -134,6 +136,9 @@ def tile_customlstmcell_kernel(
             nc.vector.tensor_scalar(out=boh[:], in0=bsum[:, 8 * G_O : 8 * G_O + 8], scalar1=0.5, scalar2=None, op0=ALU.mult)
             nc.vector.tensor_scalar(out=nbf[:], in0=bsum[:, 8 * G_F : 8 * G_F + 8], scalar1=-1.0, scalar2=None, op0=ALU.mult)
             nc.vector.tensor_scalar(out=neg_bf[:], in0=ident[:], scalar1=-1.0, scalar2=None, op0=ALU.mult)
+            nc.vector.tensor_copy(out=one_bf[:], in_=ident[:])
+            for i in range(NT):
+                nc.vector.tensor_scalar(out=neg_m[:, i, :], in0=ident[:], scalar1=m_col(i), scalar2=-1.0, op0=ALU.mult, op1=ALU.mult)
 
         def load_slab(g, c, pieces=1):
             src = W_of[g][512 * c : 512 * c + 512, :] if c < 2 else R_of[g]
@@ -143,15 +148,15 @@ def tile_customlstmcell_kernel(
                 cols = slice(k * width, k * width + width)
                 nc.sync.dma_start(out=raw[(g, c)][:, :, cols], in_=src.rearrange("(p j) w -> p j w", j=4)[:, :, cols])
 
-        def regroup(g, c, second):
-            grouped[(g, c)] = grpp.tile([P, DFF, 4], BF16, tag="grouped", name="grouped", align_bytes=64)
-            for hh in range(2):
-                dst = grouped[(g, c)][:, hh * HALF : hh * HALF + HALF, :].rearrange("p (c i) t -> p c t i", i=4)
-                view = raw[(g, c)][:, :, hh * HALF : hh * HALF + HALF].rearrange("p t (c i) -> p c t i", i=4)
-                if hh == 1 and second == "S":
-                    nc.scalar.copy(out=dst, in_=view)
-                else:
-                    nc.vector.tensor_copy(out=dst, in_=view)
+        def regroup(g, c, hh, engine):
+            if hh == 1:
+                grouped[(g, c)] = grpp.tile([P, DFF, 4], BF16, tag="grouped", name="grouped", align_bytes=64)
+            dst = grouped[(g, c)][:, hh * HALF : hh * HALF + HALF, :].rearrange("p (c i) t -> p c t i", i=4)
+            view = raw[(g, c)][:, :, hh * HALF : hh * HALF + HALF].rearrange("p t (c i) -> p c t i", i=4)
+            if engine == "S":
+                nc.scalar.copy(out=dst, in_=view)
+            else:
+                nc.vector.tensor_copy(out=dst, in_=view)
 
         def quantise(g, c):
             wq[(g, c)] = codes.tile([P, DFF], U32, name="wq%d_%d" % (g, c), align_bytes=64)
@@ -282,8 +287,9 @@ def tile_customlstmcell_kernel(
 
         def cell_hm(h, tiles):
             for i in tiles:
-                hm[(h, i)] = tmp.tile([P, HALF], F32, tag="tc", name="hm", bufs=4)
-                nc.scalar.activation(out=hm[(h, i)][:], in_=hi_sb[:, i, col_range(h)], func=ACT.Copy, scale=om[:, i : i + 1])
+                hm[(h, i)] = pstp.tile([P, HALF], F32, tag="tp", name="hm")
+                nc.tensor.matmul(out=hm[(h, i)][:], lhsT=one_bf[:], rhs=hi_sb[:, i, col_range(h)], start=True, stop=False)
+                nc.tensor.matmul(out=hm[(h, i)][:], lhsT=neg_m[:, i, :], rhs=hi_sb[:, i, col_range(h)], start=False, stop=True)
 
         def cell_h(h, pair):
             y = {}
@@ -299,8 +305,8 @@ def tile_customlstmcell_kernel(
         state_of = {"mi": Mi, "ni": Ni, "ci": Ci}
         loads = [(F, 0), (F, 1), (F, 2), (I, 0), (I, 1), (I, 2), (Z, 0), ("mi", 0), (Z, 1), ("ni", 0), ("ci", 0), (Z, 2), (O, 0), (O, 1), (O, 2)]
         slabs = [(g, c) for g in (F, I, Z, O) for c in range(3)]
-        waiting = []
-        by_vector = ((Z, 1), (O, 1))
+        by_vector = ((O, 1),)
+        step = [0]
 
         def next_load():
             while loads:
@@ -311,15 +317,20 @@ def tile_customlstmcell_kernel(
                     load_slab(what, k)
                     break
 
+        def second_half(n):
+            if n < len(slabs):
+                g, c = slabs[n]
+                regroup(g, c, 1, "V" if (g, c) in by_vector else "S")
+
         def next_slab():
-            if slabs:
-                g, c = slabs.pop(0)
-                regroup(g, c, "V" if (g, c) in by_vector else "S")
+            n = step[0]
+            step[0] = n + 1
+            second_half(n + 1)
+            if n < len(slabs):
+                regroup(slabs[n][0], slabs[n][1], 0, "V")
                 next_load()
-                waiting.append((g, c))
-            if len(waiting) > 1 or not slabs:
-                g, c = waiting.pop(0)
-                quantise(g, c)
+            if n > 0:
+                quantise(slabs[n - 1][0], slabs[n - 1][1])
 
         load_consts()
         load_x()
@@ -327,6 +338,7 @@ def tile_customlstmcell_kernel(
             next_load()
         prepare_x()
         next_load()
+        second_half(0)
         next_slab()
         next_slab()
         prepare_consts()
@@ -378,15 +390,15 @@ def tile_customlstmcell_kernel(
         cell_c(1, (0, 1))
         cell_c(1, (2, 3))
         back(O, 0)
-        cell_hm(0, (0, 1, 2, 3))
         recip_exp(0)
         leave(O, 1)
         recip_exp(1)
         cell_o(0)
-        back(O, 1)
+        cell_hm(0, (0, 1, 2, 3))
         cell_h(0, (0, 1))
         cell_h(0, (2, 3))
-        cell_hm(1, (0, 1, 2, 3))
+        back(O, 1)
         cell_o(1)
+        cell_hm(1, (0, 1, 2, 3))
         cell_h(1, (0, 1))
         cell_h(1, (2, 3))

@@ -54,7 +54,6 @@ def tile_customlstmcell_kernel(
         tmp = ctx.enter_context(tc.tile_pool(name="tmp", bufs=2))
         psmx = ctx.enter_context(tc.psum_pool(name="psmx", bufs=4))
         pstp = ctx.enter_context(tc.psum_pool(name="pstp", bufs=4))
-        ctx.enter_context(tc.manual_schedule())
 
         hi_sb = keep.tile([P, NT, DFF], BF16, name="hi_sb")
         xq = keep.tile([P, 3, TOK], U32, name="xq", align_bytes=64)

@@ -12,14 +12,17 @@ ALU = mybir.AluOpType
 ACT = mybir.ActivationFunctionType
 
 P = 128
-TOK = 512
-NT = 4
+PACK = 4
+TOKENS = 512
+TILES = TOKENS // P
 DFF = 1024
-HALF = 512
-FLOPS = 2 * 512 * 1536 * 4096
-
-G_I, G_F, G_O, G_Z = 0, 1, 2, 3
+HALF = DFF // 2
+BLOCKS = HALF // P
+PASSES = 3
 PAIRS = ((0, 1), (2, 3))
+FLOPS = 2 * TOKENS * (PASSES * P * PACK) * (4 * DFF)
+
+I, F, O, Z = 0, 1, 2, 3
 
 
 def tile_customlstmcell_kernel(
@@ -30,9 +33,10 @@ def tile_customlstmcell_kernel(
     out_0, out_1, out_2, out_3,
 ):
     nc = tc.nc
-    W_of = {G_I: WI_w, G_F: WF_w, G_O: WO_w, G_Z: WZ_w}
-    R_of = {G_I: RI_w, G_F: RF_w, G_O: RO_w, G_Z: RZ_w}
+    w_of = {I: WI_w, F: WF_w, O: WO_w, Z: WZ_w}
+    r_of = {I: RI_w, F: RF_w, O: RO_w, Z: RZ_w}
     biases = [WI_b, WF_b, WO_b, WZ_b, RI_b, RF_b, RO_b, RZ_b]
+    state_of = {"mi": Mi, "ni": Ni, "ci": Ci}
 
     def rows(ap):
         return ap.rearrange("b p k -> (b p) k")
@@ -40,278 +44,269 @@ def tile_customlstmcell_kernel(
     def tiled(ap):
         return rows(ap).rearrange("(i q) k -> q i k", q=P)
 
-    C_out, M_out, H_out, N_out = rows(out_0), rows(out_1), rows(out_2), rows(out_3)
+    c_out, m_out, h_out, n_out = rows(out_0), rows(out_1), rows(out_2), rows(out_3)
 
     with ExitStack() as ctx:
         consts = ctx.enter_context(tc.tile_pool(name="consts", bufs=1))
         keep = ctx.enter_context(tc.tile_pool(name="keep", bufs=1))
         codes = ctx.enter_context(tc.tile_pool(name="codes", bufs=1))
-        gtp = ctx.enter_context(tc.tile_pool(name="gtp", bufs=8))
-        rawp = ctx.enter_context(tc.tile_pool(name="rawp", bufs=4))
-        statep = ctx.enter_context(tc.tile_pool(name="statep", bufs=1))
-        grpp = ctx.enter_context(tc.tile_pool(name="grpp", bufs=3))
+        gate_pool = ctx.enter_context(tc.tile_pool(name="gate_pool", bufs=2 * BLOCKS))
+        raw_pool = ctx.enter_context(tc.tile_pool(name="raw_pool", bufs=4))
+        state_pool = ctx.enter_context(tc.tile_pool(name="state_pool", bufs=1))
+        grouped_pool = ctx.enter_context(tc.tile_pool(name="grouped_pool", bufs=3))
         planes = ctx.enter_context(tc.tile_pool(name="planes", bufs=1))
-        tmp = ctx.enter_context(tc.tile_pool(name="tmp", bufs=2))
-        psmx = ctx.enter_context(tc.psum_pool(name="psmx", bufs=4))
-        pstp = ctx.enter_context(tc.psum_pool(name="pstp", bufs=4))
+        pair_pool = ctx.enter_context(tc.tile_pool(name="pair_pool", bufs=2))
+        mx_banks = ctx.enter_context(tc.psum_pool(name="mx_banks", bufs=BLOCKS))
+        token_banks = ctx.enter_context(tc.psum_pool(name="token_banks", bufs=TILES))
+        ctx.enter_context(tc.manual_schedule())
 
-        hi_sb = keep.tile([P, NT, DFF], BF16, name="hi_sb")
-        xq = keep.tile([P, 3, TOK], U32, name="xq", align_bytes=64)
-        xs = keep.tile([P, 3, TOK], U8, name="xs", align_bytes=64)
+        hi_sb = keep.tile([P, TILES, DFF], BF16, name="hi_sb")
+        x_codes = keep.tile([P, PASSES, TOKENS], U32, name="x_codes", align_bytes=64)
+        x_scales = keep.tile([P, PASSES, TOKENS], U8, name="x_scales", align_bytes=64)
         ident = consts.tile([P, P], F32, name="ident")
-        braw = consts.tile([P, P], BF16, name="braw")
-        bf32 = consts.tile([P, P], F32, name="bf32")
-        cst = consts.tile([P, P], F32, name="cst")
-        bsum = consts.tile([P, 32], F32, name="bsum")
-        boh = consts.tile([P, 8], F32, name="boh")
-        om = consts.tile([P, NT], F32, name="om")
-        mh = consts.tile([P, NT], F32, name="mh")
-        nbf = consts.tile([P, 8], F32, name="nbf")
-        neg_bf = consts.tile([P, P], BF16, name="neg_bf")
-        one_bf = consts.tile([P, P], BF16, name="one_bf")
-        neg_m = consts.tile([P, NT, P], BF16, name="neg_m")
-        e1p = planes.tile([P, 8, HALF], F32, name="e1p")
-        t2p = planes.tile([P, 8, HALF], F32, name="t2p")
-        npl = planes.tile([P, 8, HALF], F32, name="npl")
-        rsp = planes.tile([P, 8, HALF], F32, name="rsp")
+        ident_bf = consts.tile([P, P], BF16, name="ident_bf")
+        neg_ident_bf = consts.tile([P, P], BF16, name="neg_ident_bf")
+        neg_m_diag = consts.tile([P, TILES, P], BF16, name="neg_m_diag")
+        vec_rows = consts.tile([P, P], BF16, name="vec_rows")
+        vec_rows_f = consts.tile([P, P], F32, name="vec_rows_f")
+        vec_cols = consts.tile([P, P], F32, name="vec_cols")
+        bias = consts.tile([P, 4 * 2 * BLOCKS], F32, name="bias")
+        neg_bias_f = consts.tile([P, 2 * BLOCKS], F32, name="neg_bias_f")
+        half_bias_o = consts.tile([P, 2 * BLOCKS], F32, name="half_bias_o")
+        one_minus_m = consts.tile([P, TILES], F32, name="one_minus_m")
+        half_m = consts.tile([P, TILES], F32, name="half_m")
 
-        raw, grouped, wq, ws, acc, gt, tp, state, hm, dif, tpi = {}, {}, {}, {}, {}, {}, {}, {}, {}, {}, {}
+        plane_a = planes.tile([P, 2 * TILES, HALF], F32, name="plane_a")
+        plane_b = planes.tile([P, 2 * TILES, HALF], F32, name="plane_b")
+        plane_c = planes.tile([P, 2 * TILES, HALF], F32, name="plane_c")
+        plane_d = planes.tile([P, 2 * TILES, HALF], F32, name="plane_d")
 
-        def m_col(i):
-            return cst[:, 64 + i : 65 + i]
+        raw, grouped, w_codes, w_scales, groups, gate_t, by_token, diff, state, rest_h = {}, {}, {}, {}, {}, {}, {}, {}, {}, {}
 
-        def col_range(h):
+        def slot(plane, h, i):
+            return plane[:, TILES * h + i, :]
+
+        def half_plane(plane, h):
+            return plane[:, TILES * h : TILES * h + TILES, :].rearrange("p a b -> p (a b)")
+
+        def m_of(i):
+            return vec_cols[:, 64 + i : 65 + i]
+
+        def half_cols(h):
             return slice(h * HALF, h * HALF + HALF)
 
-        def tok_range(i):
+        def tile_rows(i):
             return slice(i * P, i * P + P)
 
-        def load_x():
+        def load_small():
+            make_identity(nc, ident[:])
+            nc.vector.memset(vec_rows[:], 0.0)
+            for v, b in enumerate(biases):
+                nc.scalar.dma_start(out=vec_rows[8 * v : 8 * v + 8, :], in_=b.rearrange("(r c) -> r c", c=P))
+            nc.scalar.dma_start(out=vec_rows[64:68, :], in_=m.rearrange("(r x) p o -> r (x p o)", x=2))
+
+        def load_activations():
             nc.sync.dma_start(out=hi_sb[:], in_=tiled(Hi))
-            raw["zi"] = rawp.tile([P, NT, 512], BF16, tag="raw", name="zi_sb")
+            raw["zi"] = raw_pool.tile([P, TILES, 512], BF16, tag="raw", name="zi_sb")
             nc.sync.dma_start(out=raw["zi"][:], in_=tiled(Zi))
 
-        def load_consts():
-            make_identity(nc, ident[:])
-            nc.vector.memset(braw[:], 0.0)
-            for v, b in enumerate(biases):
-                nc.scalar.dma_start(out=braw[8 * v : 8 * v + 8, :], in_=b.rearrange("(r c) -> r c", c=P))
-            nc.scalar.dma_start(out=braw[64:68, :], in_=m.rearrange("(r x) p o -> r (x p o)", x=2))
-
-        def prepare_x():
-            hi_w = hi_sb[:].rearrange("q i k -> q (i k)").bitcast(F32).rearrange("q (n w u) -> q n w u", w=P, u=2)
-            zi_w = raw["zi"][:].rearrange("q i k -> q (i k)").bitcast(F32).rearrange("q (n w u) -> q n w u", w=P, u=2)
-            xg = {}
-            for c in range(3):
-                xg[c] = grpp.tile([P, 2, 1024], BF16, tag="grouped", name="xg", align_bytes=64)
-                for hh in range(2):
-                    xt = pstp.tile([P, 512], F32, tag="tp", name="xt")
+        def quantise_activations():
+            hi_words = hi_sb[:].rearrange("q i k -> q (i k)").bitcast(F32).rearrange("q (n w u) -> q n w u", w=P, u=2)
+            zi_words = raw["zi"][:].rearrange("q i k -> q (i k)").bitcast(F32).rearrange("q (n w u) -> q n w u", w=P, u=2)
+            x_grouped = {}
+            for c in range(PASSES):
+                x_grouped[c] = grouped_pool.tile([P, 2, 2 * P * PACK], BF16, tag="grouped", name="x_grouped", align_bytes=64)
+                for two in range(2):
+                    bank = token_banks.tile([P, 512], F32, tag="bank", name="x_bank")
                     for u in range(2):
-                        for il in range(2):
-                            i = 2 * hh + il
-                            src = hi_w[:, 2 * i + c, :, u] if c < 2 else zi_w[:, i, :, u]
-                            nc.tensor.transpose(xt[:, u * 256 + il * P : u * 256 + il * P + P], src, ident[:])
-                    dst = xg[c][:, hh, :].bitcast(F32).rearrange("p (r u) -> p r u", u=2)
-                    view = xt[:].rearrange("p (u r) -> p r u", u=2)
-                    if hh == 0:
-                        nc.vector.tensor_copy(out=dst, in_=view)
+                        for k in range(2):
+                            i = 2 * two + k
+                            words = hi_words[:, 2 * i + c, :, u] if c < 2 else zi_words[:, i, :, u]
+                            nc.tensor.transpose(bank[:, (2 * u + k) * P : (2 * u + k) * P + P], words, ident[:])
+                    dst = x_grouped[c][:, two, :].bitcast(F32).rearrange("p (r u) -> p r u", u=2)
+                    src = bank[:].rearrange("p (u r) -> p r u", u=2)
+                    if two == 0:
+                        nc.vector.tensor_copy(out=dst, in_=src)
                     else:
-                        nc.scalar.copy(out=dst, in_=view)
+                        nc.scalar.copy(out=dst, in_=src)
                 if c > 0:
-                    quantise_x(xg, c - 1)
-            quantise_x(xg, 2)
+                    quantise_pass(x_grouped, c - 1)
+            quantise_pass(x_grouped, PASSES - 1)
 
-        def quantise_x(xg, c):
-            nc.vector.quantize_mx(out=xq[:, c, :].bitcast(FP8X4), scales=xs[:, c, :], in_=xg[c][:].rearrange("p a b -> p (a b)"))
+        def quantise_pass(x_grouped, c):
+            nc.vector.quantize_mx(
+                out=x_codes[:, c, :].bitcast(FP8X4), scales=x_scales[:, c, :], in_=x_grouped[c][:].rearrange("p a b -> p (a b)"))
 
-        def prepare_consts():
-            nc.vector.tensor_copy(out=bf32[:], in_=braw[:])
-            bt = pstp.tile([P, 512], F32, tag="tp", name="bt")
-            nc.tensor.transpose(bt[:, 0:P], bf32[:], ident[:])
-            nc.vector.tensor_copy(out=cst[:], in_=bt[:, 0:P])
-            nc.vector.tensor_tensor(out=bsum[:], in0=cst[:, 0:32], in1=cst[:, 32:64], op=ALU.add)
-            nc.vector.tensor_scalar(out=om[:], in0=cst[:, 64:68], scalar1=-1.0, scalar2=1.0, op0=ALU.mult, op1=ALU.add)
-            nc.vector.tensor_scalar(out=mh[:], in0=cst[:, 64:68], scalar1=0.5, scalar2=None, op0=ALU.mult)
-            nc.vector.tensor_scalar(out=boh[:], in0=bsum[:, 8 * G_O : 8 * G_O + 8], scalar1=0.5, scalar2=None, op0=ALU.mult)
-            nc.vector.tensor_scalar(out=nbf[:], in0=bsum[:, 8 * G_F : 8 * G_F + 8], scalar1=-1.0, scalar2=None, op0=ALU.mult)
-            nc.vector.tensor_scalar(out=neg_bf[:], in0=ident[:], scalar1=-1.0, scalar2=None, op0=ALU.mult)
-            nc.vector.tensor_copy(out=one_bf[:], in_=ident[:])
-            for i in range(NT):
-                nc.vector.tensor_scalar(out=neg_m[:, i, :], in0=ident[:], scalar1=m_col(i), scalar2=-1.0, op0=ALU.mult, op1=ALU.mult)
+        def prepare_biases():
+            nc.vector.tensor_copy(out=vec_rows_f[:], in_=vec_rows[:])
+            bank = token_banks.tile([P, 512], F32, tag="bank", name="vec_bank")
+            nc.tensor.transpose(bank[:, 0:P], vec_rows_f[:], ident[:])
+            nc.vector.tensor_copy(out=vec_cols[:], in_=bank[:, 0:P])
+            nc.vector.tensor_tensor(out=bias[:], in0=vec_cols[:, 0:32], in1=vec_cols[:, 32:64], op=ALU.add)
+            nc.vector.tensor_scalar(out=neg_ident_bf[:], in0=ident[:], scalar1=-1.0, scalar2=None, op0=ALU.mult)
+            nc.vector.tensor_scalar(out=neg_bias_f[:], in0=bias[:, 8 * F : 8 * F + 8], scalar1=-1.0, scalar2=None, op0=ALU.mult)
 
-        def load_slab(g, c, pieces=1):
-            src = W_of[g][512 * c : 512 * c + 512, :] if c < 2 else R_of[g]
-            raw[(g, c)] = rawp.tile([P, 4, DFF], BF16, tag="raw", name="raw")
-            width = DFF // pieces
-            for k in range(pieces):
-                cols = slice(k * width, k * width + width)
-                nc.sync.dma_start(out=raw[(g, c)][:, :, cols], in_=src.rearrange("(p j) w -> p j w", j=4)[:, :, cols])
+        def prepare_blends():
+            nc.vector.tensor_scalar(out=one_minus_m[:], in0=vec_cols[:, 64:68], scalar1=-1.0, scalar2=1.0, op0=ALU.mult, op1=ALU.add)
+            nc.vector.tensor_scalar(out=half_m[:], in0=vec_cols[:, 64:68], scalar1=0.5, scalar2=None, op0=ALU.mult)
+            nc.vector.tensor_scalar(out=half_bias_o[:], in0=bias[:, 8 * O : 8 * O + 8], scalar1=0.5, scalar2=None, op0=ALU.mult)
+            nc.vector.tensor_copy(out=ident_bf[:], in_=ident[:])
+            for i in range(TILES):
+                nc.vector.tensor_scalar(out=neg_m_diag[:, i, :], in0=ident[:], scalar1=m_of(i), scalar2=-1.0, op0=ALU.mult, op1=ALU.mult)
 
-        def regroup(g, c, hh, engine):
-            if hh == 1:
-                grouped[(g, c)] = grpp.tile([P, DFF, 4], BF16, tag="grouped", name="grouped", align_bytes=64)
-            dst = grouped[(g, c)][:, hh * HALF : hh * HALF + HALF, :].rearrange("p (c i) t -> p c t i", i=4)
-            view = raw[(g, c)][:, :, hh * HALF : hh * HALF + HALF].rearrange("p t (c i) -> p c t i", i=4)
-            if engine == "S":
-                nc.scalar.copy(out=dst, in_=view)
+        def load_slab(g, c):
+            src = w_of[g][512 * c : 512 * c + 512, :] if c < 2 else r_of[g]
+            raw[(g, c)] = raw_pool.tile([P, PACK, DFF], BF16, tag="raw", name="raw")
+            nc.sync.dma_start(out=raw[(g, c)][:], in_=src.rearrange("(p j) w -> p j w", j=PACK))
+
+        def regroup(g, c, h, engine):
+            dst = grouped[(g, c)][:, half_cols(h), :].rearrange("p (c i) t -> p c t i", i=4)
+            src = raw[(g, c)][:, :, half_cols(h)].rearrange("p t (c i) -> p c t i", i=4)
+            if engine == "scalar":
+                nc.scalar.copy(out=dst, in_=src)
             else:
-                nc.vector.tensor_copy(out=dst, in_=view)
+                nc.vector.tensor_copy(out=dst, in_=src)
 
         def quantise(g, c):
-            wq[(g, c)] = codes.tile([P, DFF], U32, name="wq%d_%d" % (g, c), align_bytes=64)
-            ws[(g, c)] = codes.tile([P, DFF], U8, name="ws%d_%d" % (g, c), align_bytes=64)
+            w_codes[(g, c)] = codes.tile([P, DFF], U32, name="w_codes%d_%d" % (g, c), align_bytes=64)
+            w_scales[(g, c)] = codes.tile([P, DFF], U8, name="w_scales%d_%d" % (g, c), align_bytes=64)
             nc.vector.quantize_mx(
-                out=wq[(g, c)][:].bitcast(FP8X4), scales=ws[(g, c)][:], in_=grouped[(g, c)][:].rearrange("p w j -> p (w j)"))
+                out=w_codes[(g, c)][:].bitcast(FP8X4), scales=w_scales[(g, c)][:], in_=grouped[(g, c)][:].rearrange("p w j -> p (w j)"))
 
-        def load_state(ap, h, name):
-            state[(name, h)] = statep.tile([P, NT, HALF], BF16, tag=name, name=name)
-            nc.sync.dma_start(out=state[(name, h)][:], in_=tiled(ap)[:, :, col_range(h)])
+        def load_state(name, h):
+            state[(name, h)] = state_pool.tile([P, TILES, HALF], BF16, tag=name, name=name)
+            nc.sync.dma_start(out=state[(name, h)][:], in_=tiled(state_of[name])[:, :, half_cols(h)])
 
         def products(g, h):
-            acc[(g, h)] = []
-            for cbl in range(4):
-                cols = slice((4 * h + cbl) * P, (4 * h + cbl) * P + P)
-                a = psmx.tile([P, TOK], F32, tag="mx", name="a")
-                for c in range(3):
+            groups[(g, h)] = []
+            for b in range(BLOCKS):
+                cols = slice((BLOCKS * h + b) * P, (BLOCKS * h + b) * P + P)
+                group = mx_banks.tile([P, TOKENS], F32, tag="group", name="group")
+                for c in range(PASSES):
                     nc.tensor.matmul_mx(
-                        out=a[:],
-                        lhsT=wq[(g, c)][:, cols].bitcast(FP8X4),
-                        lhsT_scale=ws[(g, c)][:, cols],
-                        rhs=xq[:, c, :].bitcast(FP8X4),
-                        rhs_scale=xs[:, c, :],
+                        out=group[:],
+                        lhsT=w_codes[(g, c)][:, cols].bitcast(FP8X4),
+                        lhsT_scale=w_scales[(g, c)][:, cols],
+                        rhs=x_codes[:, c, :].bitcast(FP8X4),
+                        rhs_scale=x_scales[:, c, :],
                         start=(c == 0),
-                        stop=(c == 2),
+                        stop=(c == PASSES - 1),
                     )
-                acc[(g, h)].append(a)
+                groups[(g, h)].append(group)
 
-        def leave(g, h):
-            gt[(g, h)] = []
-            for cbl in range(4):
-                cb = 4 * h + cbl
-                t = gtp.tile([P, TOK], F32, tag="gt", name="t")
-                if g == G_O:
-                    nc.scalar.activation(out=t[:], in_=acc[(g, h)][cbl][:], func=ACT.Tanh, bias=boh[:, cb : cb + 1], scale=0.5)
-                elif g == G_F:
-                    nc.scalar.activation(out=t[:], in_=acc[(g, h)][cbl][:], func=ACT.Identity, bias=nbf[:, cb : cb + 1], scale=-1.0)
+        def leave_psum(g, h):
+            gate_t[(g, h)] = []
+            for b in range(BLOCKS):
+                col = BLOCKS * h + b
+                t = gate_pool.tile([P, TOKENS], F32, tag="gate_t", name="gate_t")
+                if g == O:
+                    nc.scalar.activation(out=t[:], in_=groups[(g, h)][b][:], func=ACT.Tanh, bias=half_bias_o[:, col : col + 1], scale=0.5)
+                elif g == F:
+                    nc.scalar.activation(out=t[:], in_=groups[(g, h)][b][:], func=ACT.Identity, bias=neg_bias_f[:, col : col + 1], scale=-1.0)
                 else:
-                    func = ACT.Tanh if g == G_Z else ACT.Identity
-                    nc.scalar.activation(out=t[:], in_=acc[(g, h)][cbl][:], func=func, bias=bsum[:, 8 * g + cb : 8 * g + cb + 1], scale=1.0)
-                gt[(g, h)].append(t)
+                    func = ACT.Tanh if g == Z else ACT.Identity
+                    nc.scalar.activation(out=t[:], in_=groups[(g, h)][b][:], func=func, bias=bias[:, 8 * g + col : 8 * g + col + 1], scale=1.0)
+                gate_t[(g, h)].append(t)
 
-        def back(g, h):
-            tp[(g, h)] = []
-            for i in range(NT):
-                t = pstp.tile([P, HALF], F32, tag="tp", name="t")
-                for cbl in range(4):
-                    nc.tensor.transpose(t[:, cbl * P : cbl * P + P], gt[(g, h)][cbl][:, tok_range(i)], ident[:])
-                tp[(g, h)].append(t)
+        def back(g, h, tiles):
+            for i in tiles:
+                bank = token_banks.tile([P, HALF], F32, tag="bank", name="bank")
+                for b in range(BLOCKS):
+                    nc.tensor.transpose(bank[:, b * P : b * P + P], gate_t[(g, h)][b][:, tile_rows(i)], ident[:])
+                by_token[(g, h, i)] = bank
 
         def difference(h, tiles):
             for i in tiles:
-                t = pstp.tile([P, HALF], F32, tag="tp", name="t")
-                for cbl in range(4):
-                    cols = slice(cbl * P, cbl * P + P)
-                    nc.tensor.matmul(out=t[:, cols], lhsT=gt[(G_I, h)][cbl][:, tok_range(i)], rhs=ident[:], is_transpose=True, start=True, stop=False)
-                    nc.tensor.matmul(out=t[:, cols], lhsT=gt[(G_F, h)][cbl][:, tok_range(i)], rhs=ident[:], is_transpose=True, start=False, stop=False)
-                    nc.tensor.matmul(out=t[:, cols], lhsT=neg_bf[:], rhs=state[("mi", h)][:, i, cols], start=False, stop=True)
-                dif[(h, i)] = t
+                bank = token_banks.tile([P, HALF], F32, tag="bank", name="bank")
+                for b in range(BLOCKS):
+                    cols = slice(b * P, b * P + P)
+                    nc.tensor.matmul(out=bank[:, cols], lhsT=gate_t[(I, h)][b][:, tile_rows(i)], rhs=ident[:], is_transpose=True, start=True, stop=False)
+                    nc.tensor.matmul(out=bank[:, cols], lhsT=gate_t[(F, h)][b][:, tile_rows(i)], rhs=ident[:], is_transpose=True, start=False, stop=False)
+                    nc.tensor.matmul(out=bank[:, cols], lhsT=neg_ident_bf[:], rhs=state[("mi", h)][:, i, cols], start=False, stop=True)
+                diff[(h, i)] = bank
 
-        def back_tiles(g, h, tiles):
-            for i in tiles:
-                t = pstp.tile([P, HALF], F32, tag="tp", name="t")
-                for cbl in range(4):
-                    nc.tensor.transpose(t[:, cbl * P : cbl * P + P], gt[(g, h)][cbl][:, tok_range(i)], ident[:])
-                tpi[(g, h, i)] = t
+        def rest_of_h(h):
+            for i in range(TILES):
+                bank = token_banks.tile([P, HALF], F32, tag="bank", name="bank")
+                nc.tensor.matmul(out=bank[:], lhsT=ident_bf[:], rhs=hi_sb[:, i, half_cols(h)], start=True, stop=False)
+                nc.tensor.matmul(out=bank[:], lhsT=neg_m_diag[:, i, :], rhs=hi_sb[:, i, half_cols(h)], start=False, stop=True)
+                rest_h[(h, i)] = bank
 
-        def cell_exp(h, tiles):
-            for i in tiles:
-                x = 4 * h + i
-                nc.scalar.activation(out=t2p[:, x, :], in_=dif[(h, i)][:], func=ACT.Relu, scale=-1.0)
-                nc.scalar.activation(out=npl[:, x, :], in_=dif[(h, i)][:], func=ACT.Exp, scale=-1.0)
-            for i in tiles:
-                x = 4 * h + i
-                nc.scalar.activation(out=e1p[:, x, :], in_=t2p[:, x, :], func=ACT.Exp, scale=-1.0)
+        def gates_if(h, pair):
+            for i in pair:
+                nc.scalar.activation(out=slot(plane_b, h, i), in_=diff[(h, i)][:], func=ACT.Relu, scale=-1.0)
+                nc.scalar.activation(out=slot(plane_c, h, i), in_=diff[(h, i)][:], func=ACT.Exp, scale=-1.0)
+            for i in pair:
+                nc.scalar.activation(out=slot(plane_a, h, i), in_=slot(plane_b, h, i), func=ACT.Exp, scale=-1.0)
 
-        def cell_m(h, tiles):
-            for i in tiles:
-                x = 4 * h + i
-                nc.vector.tensor_tensor(out=rsp[:, x, :], in0=tpi[(G_I, h, i)][:], in1=t2p[:, x, :], op=ALU.add)
-                nc.sync.dma_start(out=M_out[tok_range(i), col_range(h)], in_=rsp[:, x, :])
+        def cell_m(h, pair):
+            for i in pair:
+                nc.vector.tensor_tensor(out=slot(plane_d, h, i), in0=by_token[(I, h, i)][:], in1=slot(plane_b, h, i), op=ALU.add)
+                nc.sync.dma_start(out=m_out[tile_rows(i), half_cols(h)], in_=slot(plane_d, h, i))
 
         def cell_n(h, pair):
-            t1, gm = {}, {}
+            f_ni, m_f = {}, {}
             for i in pair:
-                t1[i] = tmp.tile([P, HALF], F32, tag="ta", name="t1")
-                nc.vector.scalar_tensor_tensor(out=t1[i][:], in0=npl[:, 4 * h + i, :], scalar=1.0, in1=state[("ni", h)][:, i, :], op0=ALU.min, op1=ALU.mult)
+                f_ni[i] = pair_pool.tile([P, HALF], F32, tag="first", name="f_ni")
+                nc.vector.scalar_tensor_tensor(
+                    out=f_ni[i][:], in0=slot(plane_c, h, i), scalar=1.0, in1=state[("ni", h)][:, i, :], op0=ALU.min, op1=ALU.mult)
             for i in pair:
-                gm[i] = tmp.tile([P, HALF], F32, tag="tb", name="gm")
-                nc.vector.tensor_scalar(out=gm[i][:], in0=npl[:, 4 * h + i, :], scalar1=1.0, scalar2=m_col(i), op0=ALU.min, op1=ALU.mult)
+                m_f[i] = pair_pool.tile([P, HALF], F32, tag="second", name="m_f")
+                nc.vector.tensor_scalar(out=m_f[i][:], in0=slot(plane_c, h, i), scalar1=1.0, scalar2=m_of(i), op0=ALU.min, op1=ALU.mult)
             for i in pair:
-                x = 4 * h + i
-                nc.vector.scalar_tensor_tensor(out=npl[:, x, :], in0=e1p[:, x, :], scalar=1.0, in1=t1[i][:], op0=ALU.min, op1=ALU.add)
-                nc.sync.dma_start(out=N_out[tok_range(i), col_range(h)], in_=npl[:, x, :])
+                nc.vector.tensor_tensor(out=slot(plane_c, h, i), in0=slot(plane_a, h, i), in1=f_ni[i][:], op=ALU.add)
+                nc.sync.dma_start(out=n_out[tile_rows(i), half_cols(h)], in_=slot(plane_c, h, i))
             for i in pair:
-                nc.vector.scalar_tensor_tensor(out=t2p[:, 4 * h + i, :], in0=gm[i][:], scalar=om[:, i : i + 1], in1=state[("ci", h)][:, i, :], op0=ALU.add, op1=ALU.mult)
+                nc.vector.scalar_tensor_tensor(
+                    out=slot(plane_b, h, i), in0=m_f[i][:], scalar=one_minus_m[:, i : i + 1], in1=state[("ci", h)][:, i, :], op0=ALU.add, op1=ALU.mult)
 
-        def cell_abs(h, tiles):
-            for i in tiles:
-                nc.scalar.activation(out=rsp[:, 4 * h + i, :], in_=npl[:, 4 * h + i, :], func=ACT.Abs)
+        def abs_n(h, pair):
+            for i in pair:
+                nc.scalar.activation(out=slot(plane_d, h, i), in_=slot(plane_c, h, i), func=ACT.Abs)
 
-        def half_plane(t, h):
-            return t[:, 4 * h : 4 * h + 4, :].rearrange("p a b -> p (a b)")
+        def ln_n(h):
+            nc.scalar.activation(out=half_plane(plane_d, h), in_=half_plane(plane_d, h), func=ACT.Ln)
 
-        def recip_ln(h):
-            nc.scalar.activation(out=half_plane(rsp, h), in_=half_plane(rsp, h), func=ACT.Ln)
-
-        def recip_exp(h):
-            nc.scalar.activation(out=half_plane(rsp, h), in_=half_plane(rsp, h), func=ACT.Exp, scale=-2.0)
+        def inverse_square(h):
+            nc.scalar.activation(out=half_plane(plane_d, h), in_=half_plane(plane_d, h), func=ACT.Exp, scale=-2.0)
 
         def cell_c(h, pair):
-            t3 = {}
+            i_z = {}
             for i in pair:
-                t3[i] = tmp.tile([P, HALF], F32, tag="ta", name="t3")
-                nc.vector.scalar_tensor_tensor(out=t3[i][:], in0=e1p[:, 4 * h + i, :], scalar=1.0, in1=tp[(G_Z, h)][i][:], op0=ALU.min, op1=ALU.mult)
+                i_z[i] = pair_pool.tile([P, HALF], F32, tag="first", name="i_z")
+                nc.vector.tensor_tensor(out=i_z[i][:], in0=slot(plane_a, h, i), in1=by_token[(Z, h, i)][:], op=ALU.mult)
             for i in pair:
-                x = 4 * h + i
-                nc.vector.scalar_tensor_tensor(out=e1p[:, x, :], in0=t3[i][:], scalar=m_col(i), in1=t2p[:, x, :], op0=ALU.mult, op1=ALU.add)
-                nc.sync.dma_start(out=C_out[tok_range(i), col_range(h)], in_=e1p[:, x, :])
+                nc.vector.scalar_tensor_tensor(
+                    out=slot(plane_a, h, i), in0=i_z[i][:], scalar=m_of(i), in1=slot(plane_b, h, i), op0=ALU.mult, op1=ALU.add)
+                nc.sync.dma_start(out=c_out[tile_rows(i), half_cols(h)], in_=slot(plane_a, h, i))
             for i in pair:
-                x = 4 * h + i
-                nc.vector.tensor_tensor(out=t2p[:, x, :], in0=e1p[:, x, :], in1=npl[:, x, :], op=ALU.mult)
+                nc.vector.tensor_tensor(out=slot(plane_b, h, i), in0=slot(plane_a, h, i), in1=slot(plane_c, h, i), op=ALU.mult)
 
         def cell_o(h):
-            for i in range(NT):
-                x = 4 * h + i
-                nc.vector.scalar_tensor_tensor(out=t2p[:, x, :], in0=tp[(G_O, h)][i][:], scalar=1.0, in1=t2p[:, x, :], op0=ALU.add, op1=ALU.mult)
-
-        def cell_hm(h, tiles):
-            for i in tiles:
-                hm[(h, i)] = pstp.tile([P, HALF], F32, tag="tp", name="hm")
-                nc.tensor.matmul(out=hm[(h, i)][:], lhsT=one_bf[:], rhs=hi_sb[:, i, col_range(h)], start=True, stop=False)
-                nc.tensor.matmul(out=hm[(h, i)][:], lhsT=neg_m[:, i, :], rhs=hi_sb[:, i, col_range(h)], start=False, stop=True)
+            for i in range(TILES):
+                nc.vector.scalar_tensor_tensor(
+                    out=slot(plane_b, h, i), in0=by_token[(O, h, i)][:], scalar=1.0, in1=slot(plane_b, h, i), op0=ALU.add, op1=ALU.mult)
 
         def cell_h(h, pair):
-            y = {}
+            quotient = {}
             for i in pair:
-                y[i] = tmp.tile([P, HALF], F32, tag="tb", name="y")
-                nc.vector.tensor_tensor(out=y[i][:], in0=t2p[:, 4 * h + i, :], in1=rsp[:, 4 * h + i, :], op=ALU.mult)
+                quotient[i] = pair_pool.tile([P, HALF], F32, tag="second", name="quotient")
+                nc.vector.tensor_tensor(out=quotient[i][:], in0=slot(plane_b, h, i), in1=slot(plane_d, h, i), op=ALU.mult)
             for i in pair:
-                x = 4 * h + i
-                nc.vector.scalar_tensor_tensor(out=npl[:, x, :], in0=y[i][:], scalar=mh[:, i : i + 1], in1=hm[(h, i)][:], op0=ALU.mult, op1=ALU.add)
-                nc.sync.dma_start(out=H_out[tok_range(i), col_range(h)], in_=npl[:, x, :])
+                nc.vector.scalar_tensor_tensor(
+                    out=slot(plane_c, h, i), in0=quotient[i][:], scalar=half_m[:, i : i + 1], in1=rest_h[(h, i)][:], op0=ALU.mult, op1=ALU.add)
+                nc.sync.dma_start(out=h_out[tile_rows(i), half_cols(h)], in_=slot(plane_c, h, i))
 
-        F, I, Z, O = G_F, G_I, G_Z, G_O
-        state_of = {"mi": Mi, "ni": Ni, "ci": Ci}
-        loads = [(F, 0), (F, 1), (F, 2), (I, 0), (I, 1), (I, 2), (Z, 0), ("mi", 0), (Z, 1), ("ni", 0), ("ci", 0), (Z, 2), (O, 0), (O, 1), (O, 2)]
-        slabs = [(g, c) for g in (F, I, Z, O) for c in range(3)]
-        by_vector = ((O, 1),)
+        slabs = [(g, c) for g in (F, I, Z, O) for c in range(PASSES)]
+        loads = slabs[:7] + [("mi", 0), slabs[7], ("ni", 0), ("ci", 0)] + slabs[8:]
+        whole_on_vector = (O, 1)
         step = [0]
 
         def next_load():
             while loads:
                 what, k = loads.pop(0)
                 if what in state_of:
-                    load_state(state_of[what], k, what)
+                    load_state(what, k)
                 else:
                     load_slab(what, k)
                     break
@@ -319,85 +314,85 @@ def tile_customlstmcell_kernel(
         def second_half(n):
             if n < len(slabs):
                 g, c = slabs[n]
-                regroup(g, c, 1, "V" if (g, c) in by_vector else "S")
+                grouped[(g, c)] = grouped_pool.tile([P, DFF, PACK], BF16, tag="grouped", name="grouped", align_bytes=64)
+                regroup(g, c, 1, "vector" if (g, c) == whole_on_vector else "scalar")
 
         def next_slab():
             n = step[0]
             step[0] = n + 1
             second_half(n + 1)
             if n < len(slabs):
-                regroup(slabs[n][0], slabs[n][1], 0, "V")
+                regroup(slabs[n][0], slabs[n][1], 0, "vector")
                 next_load()
             if n > 0:
                 quantise(slabs[n - 1][0], slabs[n - 1][1])
 
-        load_consts()
-        load_x()
+        load_small()
+        load_activations()
         for k in range(3):
             next_load()
-        prepare_x()
+        quantise_activations()
         next_load()
         second_half(0)
         next_slab()
         next_slab()
-        prepare_consts()
+        prepare_biases()
         next_slab()
         next_slab()
         products(F, 0)
         next_slab()
-        leave(F, 0)
+        leave_psum(F, 0)
         next_slab()
         next_slab()
         products(I, 0)
-        leave(I, 0)
+        leave_psum(I, 0)
+        prepare_blends()
 
         for h in range(2):
-            first, second = ((F, 1), (I, 1)) if h == 0 else ((Z, 0), (Z, 1))
-            difference(h, (0, 1))
-            back_tiles(I, h, (0, 1))
-            cell_exp(h, (0, 1))
+            ahead = ((F, 1), (I, 1)) if h == 0 else ((Z, 0), (Z, 1))
+            difference(h, PAIRS[0])
+            back(I, h, PAIRS[0])
+            gates_if(h, PAIRS[0])
             next_slab()
-            cell_m(h, (0, 1))
-            difference(h, (2, 3))
-            back_tiles(I, h, (2, 3))
-            cell_exp(h, (2, 3))
+            cell_m(h, PAIRS[0])
+            difference(h, PAIRS[1])
+            back(I, h, PAIRS[1])
+            gates_if(h, PAIRS[1])
             if h == 0:
-                load_state(Mi, 1, "mi")
+                load_state("mi", 1)
             next_slab()
-            products(first[0], first[1])
-            leave(first[0], first[1])
-            cell_n(h, (0, 1))
-            cell_abs(h, (0, 1))
-            next_slab()
-            cell_m(h, (2, 3))
-            products(second[0], second[1])
-            leave(second[0], second[1])
-            cell_n(h, (2, 3))
-            cell_abs(h, (2, 3))
+            for k in range(2):
+                products(ahead[k][0], ahead[k][1])
+                leave_psum(ahead[k][0], ahead[k][1])
+                cell_n(h, PAIRS[k])
+                abs_n(h, PAIRS[k])
+                if k == 0:
+                    next_slab()
+                    cell_m(h, PAIRS[1])
             if h == 0:
-                load_state(Ni, 1, "ni")
-                load_state(Ci, 1, "ci")
-        back(Z, 0)
+                load_state("ni", 1)
+                load_state("ci", 1)
+
+        back(Z, 0, range(TILES))
         products(O, 0)
-        cell_c(0, (0, 1))
-        leave(O, 0)
-        cell_c(0, (2, 3))
-        back(Z, 1)
+        cell_c(0, PAIRS[0])
+        leave_psum(O, 0)
+        cell_c(0, PAIRS[1])
+        back(Z, 1, range(TILES))
         products(O, 1)
-        recip_ln(0)
-        recip_ln(1)
-        cell_c(1, (0, 1))
-        cell_c(1, (2, 3))
-        back(O, 0)
-        recip_exp(0)
-        leave(O, 1)
-        recip_exp(1)
-        cell_o(0)
-        cell_hm(0, (0, 1, 2, 3))
-        cell_h(0, (0, 1))
-        cell_h(0, (2, 3))
-        back(O, 1)
-        cell_o(1)
-        cell_hm(1, (0, 1, 2, 3))
-        cell_h(1, (0, 1))
-        cell_h(1, (2, 3))
+        ln_n(0)
+        ln_n(1)
+        cell_c(1, PAIRS[0])
+        cell_c(1, PAIRS[1])
+        back(O, 0, range(TILES))
+        inverse_square(0)
+        leave_psum(O, 1)
+        inverse_square(1)
+
+        for h in range(2):
+            if h == 1:
+                back(O, 1, range(TILES))
+            cell_o(h)
+            rest_of_h(h)
+            cell_h(h, PAIRS[0])
+            cell_h(h, PAIRS[1])

@@ -13,16 +13,22 @@ ACT = mybir.ActivationFunctionType
 
 P = 128
 PACK = 4
+K_PASS = P * PACK
+BANK = 512
 TOKENS = 512
 TILES = TOKENS // P
 DFF = 1024
 HALF = DFF // 2
 BLOCKS = HALF // P
+GATE_BLOCKS = DFF // P
 PASSES = 3
 PAIRS = ((0, 1), (2, 3))
-FLOPS = 2 * TOKENS * (PASSES * P * PACK) * (4 * DFF)
+FLOPS = 2 * TOKENS * (PASSES * K_PASS) * (4 * DFF)
 
 I, F, O, Z = 0, 1, 2, 3
+W_COLS = 4 * GATE_BLOCKS
+M_COL = 2 * W_COLS
+FINITE = 3.3895313892515355e38
 
 
 def tile_customlstmcell_kernel(
@@ -70,9 +76,9 @@ def tile_customlstmcell_kernel(
         vec_rows = consts.tile([P, P], BF16, name="vec_rows")
         vec_rows_f = consts.tile([P, P], F32, name="vec_rows_f")
         vec_cols = consts.tile([P, P], F32, name="vec_cols")
-        bias = consts.tile([P, 4 * 2 * BLOCKS], F32, name="bias")
-        neg_bias_f = consts.tile([P, 2 * BLOCKS], F32, name="neg_bias_f")
-        half_bias_o = consts.tile([P, 2 * BLOCKS], F32, name="half_bias_o")
+        bias = consts.tile([P, W_COLS], F32, name="bias")
+        neg_bias_f = consts.tile([P, GATE_BLOCKS], F32, name="neg_bias_f")
+        half_bias_o = consts.tile([P, GATE_BLOCKS], F32, name="half_bias_o")
         one_minus_m = consts.tile([P, TILES], F32, name="one_minus_m")
         half_m = consts.tile([P, TILES], F32, name="half_m")
 
@@ -81,7 +87,8 @@ def tile_customlstmcell_kernel(
         plane_c = planes.tile([P, 2 * TILES, HALF], F32, name="plane_c")
         plane_d = planes.tile([P, 2 * TILES, HALF], F32, name="plane_d")
 
-        raw, grouped, w_codes, w_scales, groups, gate_t, by_token, diff, state, rest_h = {}, {}, {}, {}, {}, {}, {}, {}, {}, {}
+        raw, grouped, w_codes, w_scales, state = {}, {}, {}, {}, {}
+        groups, gate_t, by_token, diff, rest_h = {}, {}, {}, {}, {}
 
         def slot(plane, h, i):
             return plane[:, TILES * h + i, :]
@@ -90,7 +97,10 @@ def tile_customlstmcell_kernel(
             return plane[:, TILES * h : TILES * h + TILES, :].rearrange("p a b -> p (a b)")
 
         def m_of(i):
-            return vec_cols[:, 64 + i : 65 + i]
+            return vec_cols[:, M_COL + i : M_COL + i + 1]
+
+        def gate_bias(g):
+            return slice(GATE_BLOCKS * g, GATE_BLOCKS * g + GATE_BLOCKS)
 
         def half_cols(h):
             return slice(h * HALF, h * HALF + HALF)
@@ -98,16 +108,19 @@ def tile_customlstmcell_kernel(
         def tile_rows(i):
             return slice(i * P, i * P + P)
 
+        def keep_finite(ap):
+            nc.vector.tensor_scalar(out=ap, in0=ap, scalar1=FINITE, scalar2=-FINITE, op0=ALU.min, op1=ALU.max)
+
         def load_small():
             make_identity(nc, ident[:])
             nc.vector.memset(vec_rows[:], 0.0)
-            for v, b in enumerate(biases):
-                nc.scalar.dma_start(out=vec_rows[8 * v : 8 * v + 8, :], in_=b.rearrange("(r c) -> r c", c=P))
-            nc.scalar.dma_start(out=vec_rows[64:68, :], in_=m.rearrange("(r x) p o -> r (x p o)", x=2))
+            for v, vec in enumerate(biases):
+                nc.scalar.dma_start(out=vec_rows[gate_bias(v), :], in_=vec.rearrange("(r c) -> r c", c=P))
+            nc.scalar.dma_start(out=vec_rows[M_COL : M_COL + TILES, :], in_=m.rearrange("(r x) p o -> r (x p o)", x=2))
 
         def load_activations():
             nc.sync.dma_start(out=hi_sb[:], in_=tiled(Hi))
-            raw["zi"] = raw_pool.tile([P, TILES, 512], BF16, tag="raw", name="zi_sb")
+            raw["zi"] = raw_pool.tile([P, TILES, K_PASS], BF16, tag="raw", name="zi_sb")
             nc.sync.dma_start(out=raw["zi"][:], in_=tiled(Zi))
 
         def quantise_activations():
@@ -117,12 +130,12 @@ def tile_customlstmcell_kernel(
             for c in range(PASSES):
                 x_grouped[c] = grouped_pool.tile([P, 2, 2 * P * PACK], BF16, tag="grouped", name="x_grouped", align_bytes=64)
                 for two in range(2):
-                    bank = token_banks.tile([P, 512], F32, tag="bank", name="x_bank")
+                    bank = token_banks.tile([P, BANK], F32, tag="bank", name="x_bank")
                     for u in range(2):
-                        for k in range(2):
-                            i = 2 * two + k
+                        for which in range(2):
+                            i = 2 * two + which
                             words = hi_words[:, 2 * i + c, :, u] if c < 2 else zi_words[:, i, :, u]
-                            nc.tensor.transpose(bank[:, (2 * u + k) * P : (2 * u + k) * P + P], words, ident[:])
+                            nc.tensor.transpose(bank[:, (2 * u + which) * P : (2 * u + which) * P + P], words, ident[:])
                     dst = x_grouped[c][:, two, :].bitcast(F32).rearrange("p (r u) -> p r u", u=2)
                     src = bank[:].rearrange("p (u r) -> p r u", u=2)
                     if two == 0:
@@ -135,33 +148,39 @@ def tile_customlstmcell_kernel(
 
         def quantise_pass(x_grouped, c):
             nc.vector.quantize_mx(
-                out=x_codes[:, c, :].bitcast(FP8X4), scales=x_scales[:, c, :], in_=x_grouped[c][:].rearrange("p a b -> p (a b)"))
+                out=x_codes[:, c, :].bitcast(FP8X4),
+                scales=x_scales[:, c, :],
+                in_=x_grouped[c][:].rearrange("p a b -> p (a b)"),
+            )
 
         def prepare_biases():
             nc.vector.tensor_copy(out=vec_rows_f[:], in_=vec_rows[:])
-            bank = token_banks.tile([P, 512], F32, tag="bank", name="vec_bank")
+            bank = token_banks.tile([P, BANK], F32, tag="bank", name="vec_bank")
             nc.tensor.transpose(bank[:, 0:P], vec_rows_f[:], ident[:])
             nc.vector.tensor_copy(out=vec_cols[:], in_=bank[:, 0:P])
-            nc.vector.tensor_tensor(out=bias[:], in0=vec_cols[:, 0:32], in1=vec_cols[:, 32:64], op=ALU.add)
+            nc.vector.tensor_tensor(out=bias[:], in0=vec_cols[:, 0:W_COLS], in1=vec_cols[:, W_COLS:M_COL], op=ALU.add)
             nc.vector.tensor_scalar(out=neg_ident_bf[:], in0=ident[:], scalar1=-1.0, scalar2=None, op0=ALU.mult)
-            nc.vector.tensor_scalar(out=neg_bias_f[:], in0=bias[:, 8 * F : 8 * F + 8], scalar1=-1.0, scalar2=None, op0=ALU.mult)
+            nc.vector.tensor_scalar(out=neg_bias_f[:], in0=bias[:, gate_bias(F)], scalar1=-1.0, scalar2=None, op0=ALU.mult)
 
         def prepare_blends():
-            nc.vector.tensor_scalar(out=one_minus_m[:], in0=vec_cols[:, 64:68], scalar1=-1.0, scalar2=1.0, op0=ALU.mult, op1=ALU.add)
-            nc.vector.tensor_scalar(out=half_m[:], in0=vec_cols[:, 64:68], scalar1=0.5, scalar2=None, op0=ALU.mult)
-            nc.vector.tensor_scalar(out=half_bias_o[:], in0=bias[:, 8 * O : 8 * O + 8], scalar1=0.5, scalar2=None, op0=ALU.mult)
+            m_all = vec_cols[:, M_COL : M_COL + TILES]
+            keep_finite(m_all)
+            nc.vector.tensor_scalar(out=one_minus_m[:], in0=m_all, scalar1=-1.0, scalar2=1.0, op0=ALU.mult, op1=ALU.add)
+            nc.vector.tensor_scalar(out=half_m[:], in0=m_all, scalar1=0.5, scalar2=None, op0=ALU.mult)
+            nc.vector.tensor_scalar(out=half_bias_o[:], in0=bias[:, gate_bias(O)], scalar1=0.5, scalar2=None, op0=ALU.mult)
             nc.vector.tensor_copy(out=ident_bf[:], in_=ident[:])
             for i in range(TILES):
-                nc.vector.tensor_scalar(out=neg_m_diag[:, i, :], in0=ident[:], scalar1=m_of(i), scalar2=-1.0, op0=ALU.mult, op1=ALU.mult)
+                nc.vector.tensor_scalar(
+                    out=neg_m_diag[:, i, :], in0=ident[:], scalar1=m_of(i), scalar2=-1.0, op0=ALU.mult, op1=ALU.mult)
 
         def load_slab(g, c):
-            src = w_of[g][512 * c : 512 * c + 512, :] if c < 2 else r_of[g]
+            src = w_of[g][K_PASS * c : K_PASS * c + K_PASS, :] if c < 2 else r_of[g]
             raw[(g, c)] = raw_pool.tile([P, PACK, DFF], BF16, tag="raw", name="raw")
             nc.sync.dma_start(out=raw[(g, c)][:], in_=src.rearrange("(p j) w -> p j w", j=PACK))
 
         def regroup(g, c, h, engine):
-            dst = grouped[(g, c)][:, half_cols(h), :].rearrange("p (c i) t -> p c t i", i=4)
-            src = raw[(g, c)][:, :, half_cols(h)].rearrange("p t (c i) -> p c t i", i=4)
+            dst = grouped[(g, c)][:, half_cols(h), :].rearrange("p (n r) j -> p n j r", r=4)
+            src = raw[(g, c)][:, :, half_cols(h)].rearrange("p j (n r) -> p n j r", r=4)
             if engine == "scalar":
                 nc.scalar.copy(out=dst, in_=src)
             else:
@@ -171,7 +190,10 @@ def tile_customlstmcell_kernel(
             w_codes[(g, c)] = codes.tile([P, DFF], U32, name="w_codes%d_%d" % (g, c), align_bytes=64)
             w_scales[(g, c)] = codes.tile([P, DFF], U8, name="w_scales%d_%d" % (g, c), align_bytes=64)
             nc.vector.quantize_mx(
-                out=w_codes[(g, c)][:].bitcast(FP8X4), scales=w_scales[(g, c)][:], in_=grouped[(g, c)][:].rearrange("p w j -> p (w j)"))
+                out=w_codes[(g, c)][:].bitcast(FP8X4),
+                scales=w_scales[(g, c)][:],
+                in_=grouped[(g, c)][:].rearrange("p w j -> p (w j)"),
+            )
 
         def load_state(name, h):
             state[(name, h)] = state_pool.tile([P, TILES, HALF], BF16, tag=name, name=name)
@@ -198,15 +220,17 @@ def tile_customlstmcell_kernel(
             gate_t[(g, h)] = []
             for b in range(BLOCKS):
                 col = BLOCKS * h + b
-                t = gate_pool.tile([P, TOKENS], F32, tag="gate_t", name="gate_t")
+                block = gate_pool.tile([P, TOKENS], F32, tag="gate_t", name="gate_t")
+                group = groups[(g, h)][b]
                 if g == O:
-                    nc.scalar.activation(out=t[:], in_=groups[(g, h)][b][:], func=ACT.Tanh, bias=half_bias_o[:, col : col + 1], scale=0.5)
+                    func, scale, shift = ACT.Tanh, 0.5, half_bias_o[:, col : col + 1]
                 elif g == F:
-                    nc.scalar.activation(out=t[:], in_=groups[(g, h)][b][:], func=ACT.Identity, bias=neg_bias_f[:, col : col + 1], scale=-1.0)
+                    func, scale, shift = ACT.Identity, -1.0, neg_bias_f[:, col : col + 1]
                 else:
-                    func = ACT.Tanh if g == Z else ACT.Identity
-                    nc.scalar.activation(out=t[:], in_=groups[(g, h)][b][:], func=func, bias=bias[:, 8 * g + col : 8 * g + col + 1], scale=1.0)
-                gate_t[(g, h)].append(t)
+                    func, scale = (ACT.Tanh if g == Z else ACT.Identity), 1.0
+                    shift = bias[:, GATE_BLOCKS * g + col : GATE_BLOCKS * g + col + 1]
+                nc.scalar.activation(out=block[:], in_=group[:], func=func, bias=shift, scale=scale)
+                gate_t[(g, h)].append(block)
 
         def back(g, h, tiles):
             for i in tiles:
@@ -220,9 +244,12 @@ def tile_customlstmcell_kernel(
                 bank = token_banks.tile([P, HALF], F32, tag="bank", name="bank")
                 for b in range(BLOCKS):
                     cols = slice(b * P, b * P + P)
-                    nc.tensor.matmul(out=bank[:, cols], lhsT=gate_t[(I, h)][b][:, tile_rows(i)], rhs=ident[:], is_transpose=True, start=True, stop=False)
-                    nc.tensor.matmul(out=bank[:, cols], lhsT=gate_t[(F, h)][b][:, tile_rows(i)], rhs=ident[:], is_transpose=True, start=False, stop=False)
-                    nc.tensor.matmul(out=bank[:, cols], lhsT=neg_ident_bf[:], rhs=state[("mi", h)][:, i, cols], start=False, stop=True)
+                    a_t = gate_t[(I, h)][b][:, tile_rows(i)]
+                    neg_f_t = gate_t[(F, h)][b][:, tile_rows(i)]
+                    nc.tensor.matmul(out=bank[:, cols], lhsT=a_t, rhs=ident[:], is_transpose=True, start=True, stop=False)
+                    nc.tensor.matmul(out=bank[:, cols], lhsT=neg_f_t, rhs=ident[:], is_transpose=True, start=False, stop=False)
+                    nc.tensor.matmul(
+                        out=bank[:, cols], lhsT=neg_ident_bf[:], rhs=state[("mi", h)][:, i, cols], start=False, stop=True)
                 diff[(h, i)] = bank
 
         def rest_of_h(h):
@@ -252,13 +279,20 @@ def tile_customlstmcell_kernel(
                     out=f_ni[i][:], in0=slot(plane_c, h, i), scalar=1.0, in1=state[("ni", h)][:, i, :], op0=ALU.min, op1=ALU.mult)
             for i in pair:
                 m_f[i] = pair_pool.tile([P, HALF], F32, tag="second", name="m_f")
-                nc.vector.tensor_scalar(out=m_f[i][:], in0=slot(plane_c, h, i), scalar1=1.0, scalar2=m_of(i), op0=ALU.min, op1=ALU.mult)
+                nc.vector.tensor_scalar(
+                    out=m_f[i][:], in0=slot(plane_c, h, i), scalar1=1.0, scalar2=m_of(i), op0=ALU.min, op1=ALU.mult)
             for i in pair:
                 nc.vector.tensor_tensor(out=slot(plane_c, h, i), in0=slot(plane_a, h, i), in1=f_ni[i][:], op=ALU.add)
                 nc.sync.dma_start(out=n_out[tile_rows(i), half_cols(h)], in_=slot(plane_c, h, i))
             for i in pair:
                 nc.vector.scalar_tensor_tensor(
-                    out=slot(plane_b, h, i), in0=m_f[i][:], scalar=one_minus_m[:, i : i + 1], in1=state[("ci", h)][:, i, :], op0=ALU.add, op1=ALU.mult)
+                    out=slot(plane_b, h, i),
+                    in0=m_f[i][:],
+                    scalar=one_minus_m[:, i : i + 1],
+                    in1=state[("ci", h)][:, i, :],
+                    op0=ALU.add,
+                    op1=ALU.mult,
+                )
 
         def abs_n(h, pair):
             for i in pair:
@@ -294,7 +328,13 @@ def tile_customlstmcell_kernel(
                 nc.vector.tensor_tensor(out=quotient[i][:], in0=slot(plane_b, h, i), in1=slot(plane_d, h, i), op=ALU.mult)
             for i in pair:
                 nc.vector.scalar_tensor_tensor(
-                    out=slot(plane_c, h, i), in0=quotient[i][:], scalar=half_m[:, i : i + 1], in1=rest_h[(h, i)][:], op0=ALU.mult, op1=ALU.add)
+                    out=slot(plane_c, h, i),
+                    in0=quotient[i][:],
+                    scalar=half_m[:, i : i + 1],
+                    in1=rest_h[(h, i)][:],
+                    op0=ALU.mult,
+                    op1=ALU.add,
+                )
                 nc.sync.dma_start(out=h_out[tile_rows(i), half_cols(h)], in_=slot(plane_c, h, i))
 
         slabs = [(g, c) for g in (F, I, Z, O) for c in range(PASSES)]
@@ -304,11 +344,11 @@ def tile_customlstmcell_kernel(
 
         def next_load():
             while loads:
-                what, k = loads.pop(0)
+                what, index = loads.pop(0)
                 if what in state_of:
-                    load_state(what, k)
+                    load_state(what, index)
                 else:
-                    load_slab(what, k)
+                    load_slab(what, index)
                     break
 
         def second_half(n):
@@ -329,7 +369,7 @@ def tile_customlstmcell_kernel(
 
         load_small()
         load_activations()
-        for k in range(3):
+        for fill in range(3):
             next_load()
         quantise_activations()
         next_load()
@@ -346,7 +386,9 @@ def tile_customlstmcell_kernel(
         next_slab()
         products(I, 0)
         leave_psum(I, 0)
+        keep_finite(state[("mi", 0)][:].rearrange("p a b -> p (a b)"))
         prepare_blends()
+        keep_finite(hi_sb[:].rearrange("p a b -> p (a b)"))
 
         for h in range(2):
             ahead = ((F, 1), (I, 1)) if h == 0 else ((Z, 0), (Z, 1))
@@ -361,14 +403,16 @@ def tile_customlstmcell_kernel(
             if h == 0:
                 load_state("mi", 1)
             next_slab()
-            for k in range(2):
-                products(ahead[k][0], ahead[k][1])
-                leave_psum(ahead[k][0], ahead[k][1])
-                cell_n(h, PAIRS[k])
-                abs_n(h, PAIRS[k])
-                if k == 0:
+            for which in range(2):
+                products(ahead[which][0], ahead[which][1])
+                leave_psum(ahead[which][0], ahead[which][1])
+                cell_n(h, PAIRS[which])
+                abs_n(h, PAIRS[which])
+                if which == 0:
                     next_slab()
                     cell_m(h, PAIRS[1])
+                    if h == 0:
+                        keep_finite(state[("mi", 1)][:].rearrange("p a b -> p (a b)"))
             if h == 0:
                 load_state("ni", 1)
                 load_state("ci", 1)

from contextlib import ExitStack

from concourse import mybir
from concourse.masks import make_identity

F32 = mybir.dt.float32
BF16 = mybir.dt.bfloat16
U32 = mybir.dt.uint32
U8 = mybir.dt.uint8
FP8X4 = mybir.dt.float8_e4m3fn_x4
ALU = mybir.AluOpType
ACT = mybir.ActivationFunctionType

P = 128
PACK = 4
K_PASS = P * PACK
BANK = 512
TOKENS = 512
TILES = TOKENS // P
DFF = 1024
HALF = DFF // 2
BLOCKS = HALF // P
GATE_BLOCKS = DFF // P
PASSES = 3
PAIRS = ((0, 1), (2, 3))
FLOPS = 2 * TOKENS * (PASSES * K_PASS) * (4 * DFF)

I, F, O, Z = 0, 1, 2, 3
W_COLS = 4 * GATE_BLOCKS
M_COL = 2 * W_COLS
FINITE = 3.3895313892515355e38


def tile_customlstmcell_kernel(
    tc,
    Zi, Ci, Mi, Hi, Ni, m,
    WI_w, WI_b, WF_w, WF_b, WO_w, WO_b, WZ_w, WZ_b,
    RI_w, RI_b, RF_w, RF_b, RO_w, RO_b, RZ_w, RZ_b,
    out_0, out_1, out_2, out_3,
):
    nc = tc.nc
    w_of = {I: WI_w, F: WF_w, O: WO_w, Z: WZ_w}
    r_of = {I: RI_w, F: RF_w, O: RO_w, Z: RZ_w}
    biases = [WI_b, WF_b, WO_b, WZ_b, RI_b, RF_b, RO_b, RZ_b]
    state_of = {"mi": Mi, "ni": Ni, "ci": Ci}

    def rows(ap):
        return ap.rearrange("b p k -> (b p) k")

    def tiled(ap):
        return rows(ap).rearrange("(i q) k -> q i k", q=P)

    c_out, m_out, h_out, n_out = rows(out_0), rows(out_1), rows(out_2), rows(out_3)

    with ExitStack() as ctx:
        consts = ctx.enter_context(tc.tile_pool(name="consts", bufs=1))
        keep = ctx.enter_context(tc.tile_pool(name="keep", bufs=1))
        codes = ctx.enter_context(tc.tile_pool(name="codes", bufs=1))
        gate_pool = ctx.enter_context(tc.tile_pool(name="gate_pool", bufs=2 * BLOCKS))
        raw_pool = ctx.enter_context(tc.tile_pool(name="raw_pool", bufs=4))
        state_pool = ctx.enter_context(tc.tile_pool(name="state_pool", bufs=1))
        grouped_pool = ctx.enter_context(tc.tile_pool(name="grouped_pool", bufs=3))
        planes = ctx.enter_context(tc.tile_pool(name="planes", bufs=1))
        pair_pool = ctx.enter_context(tc.tile_pool(name="pair_pool", bufs=2))
        mx_banks = ctx.enter_context(tc.psum_pool(name="mx_banks", bufs=BLOCKS))
        token_banks = ctx.enter_context(tc.psum_pool(name="token_banks", bufs=TILES))
        ctx.enter_context(tc.manual_schedule())

        hi_sb = keep.tile([P, TILES, DFF], BF16, name="hi_sb")
        x_codes = keep.tile([P, PASSES, TOKENS], U32, name="x_codes", align_bytes=64)
        x_scales = keep.tile([P, PASSES, TOKENS], U8, name="x_scales", align_bytes=64)
        ident = consts.tile([P, P], F32, name="ident")
        ident_bf = consts.tile([P, P], BF16, name="ident_bf")
        neg_ident_bf = consts.tile([P, P], BF16, name="neg_ident_bf")
        neg_m_diag = consts.tile([P, TILES, P], BF16, name="neg_m_diag")
        vec_rows = consts.tile([P, P], BF16, name="vec_rows")
        vec_rows_f = consts.tile([P, P], F32, name="vec_rows_f")
        vec_cols = consts.tile([P, P], F32, name="vec_cols")
        bias = consts.tile([P, W_COLS], F32, name="bias")
        neg_bias_f = consts.tile([P, GATE_BLOCKS], F32, name="neg_bias_f")
        half_bias_o = consts.tile([P, GATE_BLOCKS], F32, name="half_bias_o")
        one_minus_m = consts.tile([P, TILES], F32, name="one_minus_m")
        half_m = consts.tile([P, TILES], F32, name="half_m")

        plane_a = planes.tile([P, 2 * TILES, HALF], F32, name="plane_a")
        plane_b = planes.tile([P, 2 * TILES, HALF], F32, name="plane_b")
        plane_c = planes.tile([P, 2 * TILES, HALF], F32, name="plane_c")
        plane_d = planes.tile([P, 2 * TILES, HALF], F32, name="plane_d")

        raw, grouped, w_codes, w_scales, state = {}, {}, {}, {}, {}
        groups, gate_t, by_token, diff, rest_h = {}, {}, {}, {}, {}

        def slot(plane, h, i):
            return plane[:, TILES * h + i, :]

        def half_plane(plane, h):
            return plane[:, TILES * h : TILES * h + TILES, :].rearrange("p a b -> p (a b)")

        def m_of(i):
            return vec_cols[:, M_COL + i : M_COL + i + 1]

        def gate_bias(g):
            return slice(GATE_BLOCKS * g, GATE_BLOCKS * g + GATE_BLOCKS)

        def half_cols(h):
            return slice(h * HALF, h * HALF + HALF)

        def tile_rows(i):
            return slice(i * P, i * P + P)

        def keep_finite(ap):
            nc.vector.tensor_scalar(out=ap, in0=ap, scalar1=FINITE, scalar2=-FINITE, op0=ALU.min, op1=ALU.max)

        def load_small():
            make_identity(nc, ident[:])
            nc.vector.memset(vec_rows[:], 0.0)
            for v, vec in enumerate(biases):
                nc.scalar.dma_start(out=vec_rows[gate_bias(v), :], in_=vec.rearrange("(r c) -> r c", c=P))
            nc.scalar.dma_start(out=vec_rows[M_COL : M_COL + TILES, :], in_=m.rearrange("(r x) p o -> r (x p o)", x=2))

        def load_activations():
            nc.sync.dma_start(out=hi_sb[:], in_=tiled(Hi))
            raw["zi"] = raw_pool.tile([P, TILES, K_PASS], BF16, tag="raw", name="zi_sb")
            nc.sync.dma_start(out=raw["zi"][:], in_=tiled(Zi))

        def quantise_activations():
            hi_words = hi_sb[:].rearrange("q i k -> q (i k)").bitcast(F32).rearrange("q (n w u) -> q n w u", w=P, u=2)
            zi_words = raw["zi"][:].rearrange("q i k -> q (i k)").bitcast(F32).rearrange("q (n w u) -> q n w u", w=P, u=2)
            x_grouped = {}
            for c in range(PASSES):
                x_grouped[c] = grouped_pool.tile([P, 2, 2 * P * PACK], BF16, tag="grouped", name="x_grouped", align_bytes=64)
                for two in range(2):
                    bank = token_banks.tile([P, BANK], F32, tag="bank", name="x_bank")
                    for u in range(2):
                        for which in range(2):
                            i = 2 * two + which
                            words = hi_words[:, 2 * i + c, :, u] if c < 2 else zi_words[:, i, :, u]
                            nc.tensor.transpose(bank[:, (2 * u + which) * P : (2 * u + which) * P + P], words, ident[:])
                    dst = x_grouped[c][:, two, :].bitcast(F32).rearrange("p (r u) -> p r u", u=2)
                    src = bank[:].rearrange("p (u r) -> p r u", u=2)
                    if two == 0:
                        nc.vector.tensor_copy(out=dst, in_=src)
                    else:
                        nc.scalar.copy(out=dst, in_=src)
                if c > 0:
                    quantise_pass(x_grouped, c - 1)
            quantise_pass(x_grouped, PASSES - 1)

        def quantise_pass(x_grouped, c):
            nc.vector.quantize_mx(
                out=x_codes[:, c, :].bitcast(FP8X4),
                scales=x_scales[:, c, :],
                in_=x_grouped[c][:].rearrange("p a b -> p (a b)"),
            )

        def prepare_biases():
            nc.vector.tensor_copy(out=vec_rows_f[:], in_=vec_rows[:])
            bank = token_banks.tile([P, BANK], F32, tag="bank", name="vec_bank")
            nc.tensor.transpose(bank[:, 0:P], vec_rows_f[:], ident[:])
            nc.vector.tensor_copy(out=vec_cols[:], in_=bank[:, 0:P])
            nc.vector.tensor_tensor(out=bias[:], in0=vec_cols[:, 0:W_COLS], in1=vec_cols[:, W_COLS:M_COL], op=ALU.add)
            nc.vector.tensor_scalar(out=neg_ident_bf[:], in0=ident[:], scalar1=-1.0, scalar2=None, op0=ALU.mult)
            nc.vector.tensor_scalar(out=neg_bias_f[:], in0=bias[:, gate_bias(F)], scalar1=-1.0, scalar2=None, op0=ALU.mult)

        def prepare_blends():
            m_all = vec_cols[:, M_COL : M_COL + TILES]
            keep_finite(m_all)
            nc.vector.tensor_scalar(out=one_minus_m[:], in0=m_all, scalar1=-1.0, scalar2=1.0, op0=ALU.mult, op1=ALU.add)
            nc.vector.tensor_scalar(out=half_m[:], in0=m_all, scalar1=0.5, scalar2=None, op0=ALU.mult)
            nc.vector.tensor_scalar(out=half_bias_o[:], in0=bias[:, gate_bias(O)], scalar1=0.5, scalar2=None, op0=ALU.mult)
            nc.vector.tensor_copy(out=ident_bf[:], in_=ident[:])
            for i in range(TILES):
                nc.vector.tensor_scalar(
                    out=neg_m_diag[:, i, :], in0=ident[:], scalar1=m_of(i), scalar2=-1.0, op0=ALU.mult, op1=ALU.mult)

        def load_slab(g, c):
            src = w_of[g][K_PASS * c : K_PASS * c + K_PASS, :] if c < 2 else r_of[g]
            raw[(g, c)] = raw_pool.tile([P, PACK, DFF], BF16, tag="raw", name="raw")
            nc.sync.dma_start(out=raw[(g, c)][:], in_=src.rearrange("(p j) w -> p j w", j=PACK))

        def regroup(g, c, h, engine):
            dst = grouped[(g, c)][:, half_cols(h), :].rearrange("p (n r) j -> p n j r", r=4)
            src = raw[(g, c)][:, :, half_cols(h)].rearrange("p j (n r) -> p n j r", r=4)
            if engine == "scalar":
                nc.scalar.copy(out=dst, in_=src)
            else:
                nc.vector.tensor_copy(out=dst, in_=src)

        def quantise(g, c):
            w_codes[(g, c)] = codes.tile([P, DFF], U32, name="w_codes%d_%d" % (g, c), align_bytes=64)
            w_scales[(g, c)] = codes.tile([P, DFF], U8, name="w_scales%d_%d" % (g, c), align_bytes=64)
            nc.vector.quantize_mx(
                out=w_codes[(g, c)][:].bitcast(FP8X4),
                scales=w_scales[(g, c)][:],
                in_=grouped[(g, c)][:].rearrange("p w j -> p (w j)"),
            )

        def load_state(name, h):
            state[(name, h)] = state_pool.tile([P, TILES, HALF], BF16, tag=name, name=name)
            nc.sync.dma_start(out=state[(name, h)][:], in_=tiled(state_of[name])[:, :, half_cols(h)])

        def products(g, h):
            groups[(g, h)] = []
            for b in range(BLOCKS):
                cols = slice((BLOCKS * h + b) * P, (BLOCKS * h + b) * P + P)
                group = mx_banks.tile([P, TOKENS], F32, tag="group", name="group")
                for c in range(PASSES):
                    nc.tensor.matmul_mx(
                        out=group[:],
                        lhsT=w_codes[(g, c)][:, cols].bitcast(FP8X4),
                        lhsT_scale=w_scales[(g, c)][:, cols],
                        rhs=x_codes[:, c, :].bitcast(FP8X4),
                        rhs_scale=x_scales[:, c, :],
                        start=(c == 0),
                        stop=(c == PASSES - 1),
                    )
                groups[(g, h)].append(group)

        def leave_psum(g, h):
            gate_t[(g, h)] = []
            for b in range(BLOCKS):
                col = BLOCKS * h + b
                block = gate_pool.tile([P, TOKENS], F32, tag="gate_t", name="gate_t")
                group = groups[(g, h)][b]
                if g == O:
                    func, scale, shift = ACT.Tanh, 0.5, half_bias_o[:, col : col + 1]
                elif g == F:
                    func, scale, shift = ACT.Identity, -1.0, neg_bias_f[:, col : col + 1]
                else:
                    func, scale = (ACT.Tanh if g == Z else ACT.Identity), 1.0
                    shift = bias[:, GATE_BLOCKS * g + col : GATE_BLOCKS * g + col + 1]
                nc.scalar.activation(out=block[:], in_=group[:], func=func, bias=shift, scale=scale)
                gate_t[(g, h)].append(block)

        def back(g, h, tiles):
            for i in tiles:
                bank = token_banks.tile([P, HALF], F32, tag="bank", name="bank")
                for b in range(BLOCKS):
                    nc.tensor.transpose(bank[:, b * P : b * P + P], gate_t[(g, h)][b][:, tile_rows(i)], ident[:])
                by_token[(g, h, i)] = bank

        def difference(h, tiles):
            for i in tiles:
                bank = token_banks.tile([P, HALF], F32, tag="bank", name="bank")
                for b in range(BLOCKS):
                    cols = slice(b * P, b * P + P)
                    a_t = gate_t[(I, h)][b][:, tile_rows(i)]
                    neg_f_t = gate_t[(F, h)][b][:, tile_rows(i)]
                    nc.tensor.matmul(out=bank[:, cols], lhsT=a_t, rhs=ident[:], is_transpose=True, start=True, stop=False)
                    nc.tensor.matmul(out=bank[:, cols], lhsT=neg_f_t, rhs=ident[:], is_transpose=True, start=False, stop=False)
                    nc.tensor.matmul(
                        out=bank[:, cols], lhsT=neg_ident_bf[:], rhs=state[("mi", h)][:, i, cols], start=False, stop=True)
                diff[(h, i)] = bank

        def rest_of_h(h):
            for i in range(TILES):
                bank = token_banks.tile([P, HALF], F32, tag="bank", name="bank")
                nc.tensor.matmul(out=bank[:], lhsT=ident_bf[:], rhs=hi_sb[:, i, half_cols(h)], start=True, stop=False)
                nc.tensor.matmul(out=bank[:], lhsT=neg_m_diag[:, i, :], rhs=hi_sb[:, i, half_cols(h)], start=False, stop=True)
                rest_h[(h, i)] = bank

        def gates_if(h, pair):
            for i in pair:
                nc.scalar.activation(out=slot(plane_b, h, i), in_=diff[(h, i)][:], func=ACT.Relu, scale=-1.0)
                nc.scalar.activation(out=slot(plane_c, h, i), in_=diff[(h, i)][:], func=ACT.Exp, scale=-1.0)
            for i in pair:
                nc.scalar.activation(out=slot(plane_a, h, i), in_=slot(plane_b, h, i), func=ACT.Exp, scale=-1.0)

        def cell_m(h, pair):
            for i in pair:
                nc.vector.tensor_tensor(out=slot(plane_d, h, i), in0=by_token[(I, h, i)][:], in1=slot(plane_b, h, i), op=ALU.add)
                nc.sync.dma_start(out=m_out[tile_rows(i), half_cols(h)], in_=slot(plane_d, h, i))

        def cell_n(h, pair):
            f_ni, m_f = {}, {}
            for i in pair:
                f_ni[i] = pair_pool.tile([P, HALF], F32, tag="first", name="f_ni")
                nc.vector.scalar_tensor_tensor(
                    out=f_ni[i][:], in0=slot(plane_c, h, i), scalar=1.0, in1=state[("ni", h)][:, i, :], op0=ALU.min, op1=ALU.mult)
            for i in pair:
                m_f[i] = pair_pool.tile([P, HALF], F32, tag="second", name="m_f")
                nc.vector.tensor_scalar(
                    out=m_f[i][:], in0=slot(plane_c, h, i), scalar1=1.0, scalar2=m_of(i), op0=ALU.min, op1=ALU.mult)
            for i in pair:
                nc.vector.tensor_tensor(out=slot(plane_c, h, i), in0=slot(plane_a, h, i), in1=f_ni[i][:], op=ALU.add)
                nc.sync.dma_start(out=n_out[tile_rows(i), half_cols(h)], in_=slot(plane_c, h, i))
            for i in pair:
                nc.vector.scalar_tensor_tensor(
                    out=slot(plane_b, h, i),
                    in0=m_f[i][:],
                    scalar=one_minus_m[:, i : i + 1],
                    in1=state[("ci", h)][:, i, :],
                    op0=ALU.add,
                    op1=ALU.mult,
                )

        def abs_n(h, pair):
            for i in pair:
                nc.scalar.activation(out=slot(plane_d, h, i), in_=slot(plane_c, h, i), func=ACT.Abs)

        def ln_n(h):
            nc.scalar.activation(out=half_plane(plane_d, h), in_=half_plane(plane_d, h), func=ACT.Ln)

        def inverse_square(h):
            nc.scalar.activation(out=half_plane(plane_d, h), in_=half_plane(plane_d, h), func=ACT.Exp, scale=-2.0)

        def cell_c(h, pair):
            i_z = {}
            for i in pair:
                i_z[i] = pair_pool.tile([P, HALF], F32, tag="first", name="i_z")
                nc.vector.tensor_tensor(out=i_z[i][:], in0=slot(plane_a, h, i), in1=by_token[(Z, h, i)][:], op=ALU.mult)
            for i in pair:
                nc.vector.scalar_tensor_tensor(
                    out=slot(plane_a, h, i), in0=i_z[i][:], scalar=m_of(i), in1=slot(plane_b, h, i), op0=ALU.mult, op1=ALU.add)
                nc.sync.dma_start(out=c_out[tile_rows(i), half_cols(h)], in_=slot(plane_a, h, i))
            for i in pair:
                nc.vector.tensor_tensor(out=slot(plane_b, h, i), in0=slot(plane_a, h, i), in1=slot(plane_c, h, i), op=ALU.mult)

        def cell_o(h):
            for i in range(TILES):
                nc.vector.scalar_tensor_tensor(
                    out=slot(plane_b, h, i), in0=by_token[(O, h, i)][:], scalar=1.0, in1=slot(plane_b, h, i), op0=ALU.add, op1=ALU.mult)

        def cell_h(h, pair):
            quotient = {}
            for i in pair:
                quotient[i] = pair_pool.tile([P, HALF], F32, tag="second", name="quotient")
                nc.vector.tensor_tensor(out=quotient[i][:], in0=slot(plane_b, h, i), in1=slot(plane_d, h, i), op=ALU.mult)
            for i in pair:
                nc.vector.scalar_tensor_tensor(
                    out=slot(plane_c, h, i),
                    in0=quotient[i][:],
                    scalar=half_m[:, i : i + 1],
                    in1=rest_h[(h, i)][:],
                    op0=ALU.mult,
                    op1=ALU.add,
                )
                nc.sync.dma_start(out=h_out[tile_rows(i), half_cols(h)], in_=slot(plane_c, h, i))

        slabs = [(g, c) for g in (F, I, Z, O) for c in range(PASSES)]
        loads = slabs[:7] + [("mi", 0), slabs[7], ("ni", 0), ("ci", 0)] + slabs[8:]
        whole_on_vector = (O, 1)
        step = [0]

        def next_load():
            while loads:
                what, index = loads.pop(0)
                if what in state_of:
                    load_state(what, index)
                else:
                    load_slab(what, index)
                    break

        def second_half(n):
            if n < len(slabs):
                g, c = slabs[n]
                grouped[(g, c)] = grouped_pool.tile([P, DFF, PACK], BF16, tag="grouped", name="grouped", align_bytes=64)
                regroup(g, c, 1, "vector" if (g, c) == whole_on_vector else "scalar")

        def next_slab():
            n = step[0]
            step[0] = n + 1
            second_half(n + 1)
            if n < len(slabs):
                regroup(slabs[n][0], slabs[n][1], 0, "vector")
                next_load()
            if n > 0:
                quantise(slabs[n - 1][0], slabs[n - 1][1])

        load_small()
        load_activations()
        for fill in range(3):
            next_load()
        quantise_activations()
        next_load()
        second_half(0)
        next_slab()
        next_slab()
        prepare_biases()
        next_slab()
        next_slab()
        products(F, 0)
        next_slab()
        leave_psum(F, 0)
        next_slab()
        next_slab()
        products(I, 0)
        leave_psum(I, 0)
        keep_finite(state[("mi", 0)][:].rearrange("p a b -> p (a b)"))
        prepare_blends()
        keep_finite(hi_sb[:].rearrange("p a b -> p (a b)"))

        for h in range(2):
            ahead = ((F, 1), (I, 1)) if h == 0 else ((Z, 0), (Z, 1))
            difference(h, PAIRS[0])
            back(I, h, PAIRS[0])
            gates_if(h, PAIRS[0])
            next_slab()
            cell_m(h, PAIRS[0])
            difference(h, PAIRS[1])
            back(I, h, PAIRS[1])
            gates_if(h, PAIRS[1])
            if h == 0:
                load_state("mi", 1)
            next_slab()
            for which in range(2):
                products(ahead[which][0], ahead[which][1])
                leave_psum(ahead[which][0], ahead[which][1])
                cell_n(h, PAIRS[which])
                abs_n(h, PAIRS[which])
                if which == 0:
                    next_slab()
                    cell_m(h, PAIRS[1])
                    if h == 0:
                        keep_finite(state[("mi", 1)][:].rearrange("p a b -> p (a b)"))
            if h == 0:
                load_state("ni", 1)
                load_state("ci", 1)

        back(Z, 0, range(TILES))
        products(O, 0)
        cell_c(0, PAIRS[0])
        leave_psum(O, 0)
        cell_c(0, PAIRS[1])
        back(Z, 1, range(TILES))
        products(O, 1)
        ln_n(0)
        ln_n(1)
        cell_c(1, PAIRS[0])
        cell_c(1, PAIRS[1])
        back(O, 0, range(TILES))
        inverse_square(0)
        leave_psum(O, 1)
        inverse_square(1)

        for h in range(2):
            if h == 1:
                back(O, 1, range(TILES))
            cell_o(h)
            rest_of_h(h)
            cell_h(h, PAIRS[0])
            cell_h(h, PAIRS[1])
